import numpy as np
import ml_dtypes


def mxq(x, axis, fmt="e4m3"):
    dtype, down = {"e4m3": (ml_dtypes.float8_e4m3fn, 7), "e5m2": (ml_dtypes.float8_e5m2, 14)}[fmt]
    v = np.moveaxis(np.asarray(x, np.float32).astype(ml_dtypes.bfloat16).astype(np.float64), axis, -1)
    blocks = v.reshape(v.shape[:-1] + (-1, 32))
    amax = np.abs(blocks).max(-1, keepdims=True)
    byte = np.maximum(np.where(amax > 0, np.frexp(amax)[1] - 1 + 127, 0) - down, 1)
    scale = np.exp2(byte - 127.0)
    codes = (blocks / scale).astype(np.float32).astype(dtype).astype(np.float64)
    return np.moveaxis((codes * scale).reshape(v.shape), -1, axis)


WIDE = False


def mx_kscale(k):
    if not WIDE:
        return np.ones(k)
    levels = np.array([10, -10, 5, -5, 0])
    if k % 512:
        return np.exp2(np.random.permutation(np.resize(levels, k // 32))).repeat(32)
    a = np.empty((k // 512, 16))
    for p in range(k // 512):
        a[p, :8] = np.random.permutation(np.resize(levels, 8))
        for g in range(8):
            far = levels[np.abs(levels - a[p, g]) >= 10]
            a[p, g + 8] = far[np.random.randint(len(far))]
    return np.exp2(a.ravel()).repeat(32)


BF16 = ml_dtypes.bfloat16


def bf(x):
    return np.asarray(x, np.float32).astype(BF16)


def f64(x):
    return np.asarray(x).astype(np.float64)


B, T, D, H, HK, HD, W = 2, 1024, 1024, 8, 2, 128, 512
HALF = HD // 2
ROPE_BASE = 10000.0
EPS = 1e-6


def rope_cos_sin():
    inv_freq = 1.0 / ROPE_BASE ** (np.arange(0, HD, 2) / HD)
    freqs = np.arange(T)[:, None] * inv_freq[None, :]
    emb = np.concatenate([freqs, freqs], axis=-1)
    return np.cos(emb), np.sin(emb)


def rotate_half(u):
    return np.concatenate([-u[..., HALF:], u[..., :HALF]], axis=-1)


def heads(u, n):
    return u.reshape(B, T, n, HD).transpose(0, 2, 1, 3)


def l2_gain(u, gamma):
    return u / (np.sqrt((u * u).sum(-1, keepdims=True)) + EPS) * gamma


def draw0():
    s = mx_kscale(D)
    return {"x": bf(np.random.standard_normal((B, T, D)) * s),
            "wq": bf(np.random.standard_normal((H * HD, D)) / np.sqrt(D) / s[None, :]),
            "wk": bf(np.random.standard_normal((HK * HD, D)) / np.sqrt(D) / s[None, :]),
            "wv": bf(np.random.standard_normal((HK * HD, D)) * 2.0 / np.sqrt(D) / s[None, :]),
            "gamma_q": bf(np.sqrt(HD) * (1.0 + 0.1 * np.random.standard_normal(HD))),
            "gamma_k": bf(np.sqrt(HD) * (1.0 + 0.1 * np.random.standard_normal(HD)))}


def core(x, wq, wk, wv, gamma_q, gamma_k):
    xq = mxq(f64(x), 2, "e4m3")
    q = heads(xq @ mxq(f64(wq), 1, "e4m3").T, H)
    k = heads(xq @ mxq(f64(wk), 1, "e4m3").T, HK)
    v = heads(xq @ mxq(f64(wv), 1, "e4m3").T, HK)
    cos, sin = rope_cos_sin()
    q = q * cos + rotate_half(q) * sin
    k = k * cos + rotate_half(k) * sin
    q = l2_gain(q, f64(gamma_q))
    k = l2_gain(k, f64(gamma_k))
    return q, k, v


def e4m3fn_bytes(y):
    return np.clip(np.asarray(y, np.float64), -448.0, 448.0).astype(np.float32).astype(ml_dtypes.float8_e4m3fn).view(np.uint8)


def e4m3fn_values(b):
    return np.asarray(b, np.uint8).view(ml_dtypes.float8_e4m3fn).astype(np.float64)


def setup_inputs():
    d = draw0()
    x0 = np.asarray(d['x']).astype(np.float64)
    s = (np.max(np.abs(x0), axis=(0, 1), keepdims=True) / 448.0).astype(np.float32)
    out = {}
    for k, v in d.items():
        if k == 'x':
            out['x_bytes'] = e4m3fn_bytes(x0 / s.astype(np.float64))
            out['x_scale'] = s
        else:
            out[k] = v
    return out


def reference(x_bytes, x_scale, wq, wk, wv, gamma_q, gamma_k):
    return core(e4m3fn_values(x_bytes) * x_scale.astype(np.float64), wq, wk, wv, gamma_q, gamma_k)

@@ -1,0 +1,368 @@
+from contextlib import ExitStack
+
+import concourse.mybir as mybir
+from concourse.masks import make_identity
+
+F32 = mybir.dt.float32
+BF16 = mybir.dt.bfloat16
+U32 = mybir.dt.uint32
+U8 = mybir.dt.uint8
+I32 = mybir.dt.int32
+FP8 = mybir.dt.float8_e4m3fn
+FP8X4 = mybir.dt.float8_e4m3fn_x4
+ALU = mybir.AluOpType
+ACT = mybir.ActivationFunctionType
+
+P = 128
+D = 1024
+HD = 128
+HALF = 64
+ROPE_BASE = 10000.0
+EPS = 1e-6
+GROUPS = 8
+BANKS = 3
+UNITS = 48
+LEAD = 4
+LAG = 3
+TWO_PI = 6.283185307179586
+
+FLOPS = 2 * 2048 * 1024 * 1536
+
+
+def tile_gqaattention_pa_kernel(tc, x_bytes, x_scale, wq, wk, wv, gamma_q, gamma_k, out_0, out_1, out_2):
+    nc = tc.nc
+    with ExitStack() as ctx:
+        keep = ctx.enter_context(tc.tile_pool(name="keep", bufs=1))
+        rings = ctx.enter_context(tc.tile_pool(name="rings", bufs=1))
+        banks = ctx.enter_context(tc.psum_pool(name="banks", bufs=1))
+        taken = {}
+
+        def ring(pool, base, depth, shape, dtype, align=None):
+            k = taken.get(base, 0)
+            taken[base] = k + 1
+            slot = "%s%d" % (base, k % depth)
+            if align is None:
+                return pool.tile(shape, dtype, name=slot)
+            return pool.tile(shape, dtype, name=slot, align_bytes=align)
+
+        one = keep.tile([P, 1], F32, name="one")
+        nc.vector.memset(one[:], 1.0)
+        first = keep.tile([P, 1], F32, name="first")
+        nc.scalar.activation(out=first[:], in_=one[:], func=ACT.Sin)
+
+        xb = keep.tile([P, GROUPS, 2 * D], U8, name="x_bytes_sb")
+        x_rows = x_bytes.rearrange("b t k -> (b t) k").rearrange("(g p i) k -> p g (i k)", p=P, i=2)
+        scale_t = keep.tile([P, 2, 4], F32, name="scale_t")
+        wraw = keep.tile([P, 12, D], BF16, name="wraw")
+        gam_rows = keep.tile([P, 2 * HD], BF16, name="gam_rows")
+        nc.vector.memset(gam_rows[:], 0.0)
+        ones_sq = keep.tile([P, P], BF16, name="ones_sq")
+        nc.vector.memset(ones_sq[:], 1.0)
+        gam = keep.tile([P, 2, HD], F32, name="gam")
+        wq_rows = wq.rearrange("(a p) k -> p a k", p=P)
+
+        nc.sync.dma_start(out=xb[:, 0:1, :], in_=x_rows[:, 0:1, :])
+        with nc.allow_non_contiguous_dma(reason="four scales to a partition and pass"):
+            nc.sync.dma_start(out=scale_t[:], in_=x_scale.rearrange("a b (c p t) -> p (a b c) t", p=P, t=4))
+        nc.sync.dma_start(out=gam_rows[0:1, 0:HD], in_=gamma_q.unsqueeze(0))
+        nc.sync.dma_start(out=gam_rows[0:1, HD:2 * HD], in_=gamma_k.unsqueeze(0))
+        nc.sync.dma_start(out=wraw[:, 0:2, :], in_=wq_rows[:, 0:2, :])
+        nc.sync.dma_start(out=wraw[:, 2:4, :], in_=wq_rows[:, 2:4, :])
+        nc.sync.dma_start(out=xb[:, 1:2, :], in_=x_rows[:, 1:2, :])
+        nc.sync.dma_start(out=wraw[:, 4:8, :], in_=wq_rows[:, 4:8, :])
+        nc.sync.dma_start(out=wraw[:, 8:10, :], in_=wk.rearrange("(a p) k -> p a k", p=P))
+        nc.sync.dma_start(out=wraw[:, 10:12, :], in_=wv.rearrange("(a p) k -> p a k", p=P))
+        nc.sync.dma_start(out=xb[:, 2:4, :], in_=x_rows[:, 2:4, :])
+        nc.sync.dma_start(out=xb[:, 4:8, :], in_=x_rows[:, 4:8, :])
+
+        tpos = keep.tile([P, 8], F32, name="tpos")
+        nc.gpsimd.iota(tpos[:], pattern=[[256, 4], [1, 2]], base=0, channel_multiplier=2,
+                       allow_small_or_imprecise_dtypes=True)
+        ident = keep.tile([P, P], F32, name="ident")
+        make_identity(nc, ident[:])
+
+        gam_ps = ring(banks, "tp", 2, [P, 2, 2, P], F32)
+        nc.tensor.matmul(out=gam_ps[:, 0].rearrange("p u r -> p (u r)"), lhsT=ones_sq[:], rhs=gam_rows[:], start=True, stop=True)
+        nc.scalar.copy(out=gam[:].rearrange("p w d -> p (w d)"), in_=gam_ps[:, 0].rearrange("p u r -> p (u r)"))
+
+
+        turns = keep.tile([P, 8], F32, name="turns")
+        nc.vector.tensor_scalar(out=turns[:], in0=tpos[:], scalar1=1.0 / TWO_PI, scalar2=None, op0=ALU.mult)
+        freq = keep.tile([P, HALF], F32, name="freq")
+        nc.vector.memset(freq[:, 0:1], 1.0)
+        for m in (1, 2, 4, 8, 16, 32):
+            nc.vector.tensor_scalar(out=freq[:, m:2 * m], in0=freq[:, 0:m], scalar1=ROPE_BASE ** (-m / HALF),
+                                    scalar2=None, op0=ALU.mult)
+        phi = keep.tile([P, 8, HALF], F32, name="phi")
+        nc.vector.tensor_tensor(out=phi[:], in0=turns[:].unsqueeze(2).to_broadcast([P, 8, HALF]),
+                                in1=freq[:].unsqueeze(1).to_broadcast([P, 8, HALF]), op=ALU.mult)
+        whole_i = keep.tile([P, 8 * HALF], I32, name="whole_i")
+        phi_f = phi[:].rearrange("p a j -> p (a j)")
+        nc.vector.tensor_copy(out=whole_i[:], in_=phi_f)
+        whole = keep.tile([P, 8 * HALF], F32, name="whole")
+        nc.vector.tensor_copy(out=whole[:], in_=whole_i[:])
+        frac = keep.tile([P, 8 * HALF], F32, name="frac")
+        nc.vector.tensor_tensor(out=frac[:], in0=phi_f, in1=whole[:], op=ALU.subtract)
+        negs = keep.tile([P, 8, HALF], F32, name="negs")
+        negs_f = negs[:].rearrange("p a j -> p (a j)")
+        nc.vector.scalar_tensor_tensor(out=negs_f, in0=frac[:], scalar=0.5, in1=frac[:], op0=ALU.is_gt,
+                                       op1=ALU.subtract)
+        cq = keep.tile([P, 8 * HALF], F32, name="cq")
+        nc.vector.tensor_scalar(out=cq[:], in0=negs_f, scalar1=-1.0, scalar2=0.25, op0=ALU.mult, op1=ALU.add)
+        negc = keep.tile([P, 8, HALF], F32, name="negc")
+        nc.vector.scalar_tensor_tensor(out=negc[:].rearrange("p a j -> p (a j)"), in0=cq[:], scalar=0.5, in1=cq[:],
+                                       op0=ALU.is_gt, op1=ALU.subtract)
+        cos_t = keep.tile([P, 8, HALF], F32, name="cos_t")
+        sin2 = keep.tile([P, 8, 2, HALF], F32, name="sin2")
+        rope = keep.tile([P, 2, 2, 8, HD], F32, name="rope")
+
+        def sines():
+            nc.scalar.activation(out=cos_t[:], in_=negc[:], func=ACT.Sin, scale=-TWO_PI)
+            nc.scalar.activation(out=sin2[:, :, 0, :], in_=negs[:], func=ACT.Sin, scale=TWO_PI)
+            nc.scalar.activation(out=sin2[:, :, 1, :], in_=negs[:], func=ACT.Sin, scale=-TWO_PI)
+
+        def gains(a):
+            gis = slice(2 * a, 2 * a + 2)
+            for w in range(2):
+                gv = gam[:, w, :].rearrange("p (s j) -> p s j", s=2).unsqueeze(1).to_broadcast([P, 2, 2, HALF])
+                nc.gpsimd.tensor_tensor(
+                    out=rope[:, w, 0, gis, :].rearrange("p a (s j) -> p a s j", s=2),
+                    in0=cos_t[:, gis, :].unsqueeze(2).to_broadcast([P, 2, 2, HALF]), in1=gv, op=ALU.mult)
+                nc.gpsimd.tensor_tensor(
+                    out=rope[:, w, 1, gis, :].rearrange("p a (s j) -> p a s j", s=2),
+                    in0=sin2[:, gis, :, :], in1=gv, op=ALU.mult)
+
+        wc = keep.tile([P, 2, 1536], U32, name="wc", align_bytes=64)
+        wsc = keep.tile([P, 2, 1536], U8, name="wsc", align_bytes=64)
+
+        def turn_words(words, dst):
+            t = ring(banks, "tp", 2, [P, 2, 2, P], F32)
+            for c in range(2):
+                for u in range(2):
+                    nc.tensor.transpose(t[:, c, u, :], words[:, 256 * c + u:256 * (c + 1):2], ident[:])
+            nc.scalar.copy(out=dst, in_=t[:].rearrange("p c u r -> p c r u"))
+
+        def wturn(b):
+            wg = ring(rings, "wg", 2, [P, 2, 512, 2], F32, 64)
+            for al in range(4):
+                turn_words(wraw[:, 4 * b + al, :].bitcast(F32), wg[:, :, P * al:P * (al + 1), :])
+            return wg
+
+        def wquant(b, wg):
+            for c in range(2):
+                cols = slice(512 * b, 512 * (b + 1))
+                nc.vector.quantize_mx(out=wc[:, c, cols].bitcast(FP8X4), scales=wsc[:, c, cols],
+                                      in_=wg[:, c].rearrange("p f u -> p (f u)").bitcast(BF16))
+
+        def widen(g):
+            xs = ring(rings, "xs", 2, [P, 2, D], BF16)
+            for i in range(2):
+                nc.scalar.copy(out=xs[:, i, :], in_=xb[:, g, D * i:D * (i + 1)].bitcast(FP8))
+            return xs
+
+        def turn(xs):
+            ts = []
+            for i in range(2):
+                words = xs[:, i, :].bitcast(F32)
+                t = ring(banks, "tp", 2, [P, 2, 2, P], F32)
+                for c in range(2):
+                    for u in range(2):
+                        nc.tensor.transpose(t[:, c, u, :], words[:, 256 * c + u:256 * (c + 1):2], ident[:])
+                ts.append(t)
+            return ts
+
+        def scaled(ts):
+            xg = ring(rings, "xg", 2, [P, 2, 2, P, 4], BF16, 64)
+            for i in range(2):
+                t = ts[i]
+                for c in range(2):
+                    nc.vector.tensor_tensor(
+                        out=xg[:, i, c].rearrange("p r (u e) -> p r u e", u=2),
+                        in0=scale_t[:, c, :].rearrange("p (u e) -> p u e", u=2).unsqueeze(1).to_broadcast([P, P, 2, 2]),
+                        in1=t[:, c].rearrange("p u r -> p (u r)").bitcast(BF16).rearrange("p (u r e) -> p r u e", u=2, e=2),
+                        op=ALU.mult)
+            return xg
+
+        def quant(xg):
+            xc = ring(rings, "xc", 4, [P, 512], U32, 64)
+            xsc = ring(rings, "xsc", 4, [P, 512], U8, 64)
+            nc.vector.quantize_mx(out=xc[:].bitcast(FP8X4), scales=xsc[:],
+                                  in_=xg[:].rearrange("p i c r t -> p (i c r t)"))
+            return xc, xsc
+
+        q_dst = [out_0[bt].rearrange("h (a p i) d -> a p h (i d)", a=4, p=P, i=2) for bt in range(2)]
+        k_dst = [out_1[bt].rearrange("h (a p i) d -> a p h (i d)", a=4, p=P, i=2) for bt in range(2)]
+        v_dst = [out_2[bt].rearrange("h (a p i) d -> a p h (i d)", a=4, p=P, i=2) for bt in range(2)]
+
+        xs_of = {}
+        xg_of = {}
+        tp_of = {}
+        xq = {}
+        un = {}
+        pr = {}
+        ot = {}
+
+        def where(m):
+            g, r = divmod(m, 6)
+            b, i = divmod(r, 2)
+            return g, b, i, (4 if b < 2 else 2)
+
+        def mx(m):
+            g, b, i, nh = where(m)
+            xc, xsc = xq[g]
+            acc = ring(banks, "acc", 6, [P, 512], F32)
+            for c in range(2):
+                lc = slice(256 * i + P * c, 256 * i + P * (c + 1))
+                rc = slice(512 * b, 512 * (b + 1))
+                nc.tensor.matmul_mx(out=acc[:], lhsT=xc[:, lc].bitcast(FP8X4), lhsT_scale=xsc[:, lc],
+                                    rhs=wc[:, c, rc].bitcast(FP8X4), rhs_scale=wsc[:, c, rc],
+                                    start=(c == 0), stop=(c == 1))
+            un[m] = {"acc": acc}
+
+        def rope_mul(m):
+            g, b, i, nh = where(m)
+            gi = 2 * (g % 4) + i
+            acc = un[m]["acc"]
+            t1 = ring(rings, "ta", 4, [P, 4, HD], F32)
+            t2 = ring(rings, "tb", 4, [P, 4, HD], F32)
+            swapped = acc[:, 0:nh * HD].rearrange("p (h s j) -> p h s j", s=2, j=HALF)[:, :, ::-1, :]
+            if b < 2:
+                nc.vector.tensor_tensor(out=t1[:], in0=rope[:, 0, 0, gi, :].unsqueeze(1).to_broadcast([P, nh, HD]),
+                                        in1=acc[:].rearrange("p (h d) -> p h d", d=HD), op=ALU.mult)
+                nc.vector.tensor_tensor(
+                    out=t2[:].rearrange("p h (s j) -> p h s j", s=2),
+                    in0=rope[:, 0, 1, gi, :].rearrange("p (s j) -> p s j", s=2).unsqueeze(1).to_broadcast(
+                        [P, nh, 2, HALF]),
+                    in1=swapped, op=ALU.mult)
+            else:
+                rinv = pr[(g, 1)]["rinv"]
+                for h in range(nh):
+                    col = rinv[:, i * nh + h:i * nh + h + 1]
+                    nc.vector.scalar_tensor_tensor(out=t1[:, h, :], in0=acc[:, HD * h:HD * (h + 1)], scalar=col,
+                                                   in1=rope[:, 1, 0, gi, :], op0=ALU.mult, op1=ALU.mult)
+                    nc.vector.scalar_tensor_tensor(out=t2[:, h, :].rearrange("p (s j) -> p s j", s=2),
+                                                   in0=swapped[:, h], scalar=col,
+                                                   in1=rope[:, 1, 1, gi, :].rearrange("p (s j) -> p s j", s=2),
+                                                   op0=ALU.mult, op1=ALU.mult)
+            un[m]["t1"] = t1
+            un[m]["t2"] = t2
+
+        def rope_add(m):
+            g, b, i, nh = where(m)
+            if b < 2:
+                rot = ring(rings, "rot", 6, [P, nh, HD], F32)
+                un[m]["rot"] = rot
+                dst = rot[:]
+            else:
+                dst = ot[(g, b)][:, 0:2, i, :]
+            nc.gpsimd.tensor_tensor(out=dst, in0=un[m]["t1"][:, 0:nh], in1=un[m]["t2"][:, 0:nh], op=ALU.add)
+
+        def norms(m):
+            g, b, i, nh = where(m)
+            kind = 0 if b < 2 else 1
+            if i == 0:
+                o = ring(rings, "o", 6, [P, 4, 2, HD], F32)
+                ot[(g, b)] = o
+            if i == 0 and b != 1:
+                ss = ring(rings, "ss", 4, [P, 16], F32)
+                pr[(g, kind)] = {"ss": ss}
+            ss = pr[(g, kind)]["ss"]
+            acc = un[m]["acc"]
+            base = (b % 2) * 8 + i * nh
+            for h in range(nh):
+                junk = ring(rings, "junk", 4, [P, HD], BF16)
+                nc.scalar.activation(out=junk[:], in_=acc[:, HD * h:HD * (h + 1)], func=ACT.Square,
+                                     accum_out=ss[:, base + h:base + h + 1])
+            if b == 2:
+                nc.scalar.copy(out=ot[(g, b)][:, 2:4, i, :], in_=acc[:, 256:512].rearrange("p (h d) -> p h d", d=HD))
+
+        def root(g, kind):
+            n = 4 if kind else 16
+            nrm = ring(rings, "nrm", 4, [P, 16], F32)
+            nc.scalar.activation(out=nrm[:, 0:n], in_=pr[(g, kind)]["ss"][:, 0:n], func=ACT.Sqrt)
+            pr[(g, kind)]["nrm"] = nrm
+
+        def plus_eps(g, kind):
+            n = 4 if kind else 16
+            nrm_e = ring(rings, "nrme", 4, [P, 16], F32)
+            nc.scalar.activation(out=nrm_e[:, 0:n], in_=pr[(g, kind)]["nrm"][:, 0:n], func=ACT.Copy, bias=EPS)
+            pr[(g, kind)]["nrm_e"] = nrm_e
+
+        def invert(g, kind):
+            n = 4 if kind else 16
+            rinv = ring(rings, "rinv", 4, [P, 16], F32)
+            nc.vector.reciprocal(out=rinv[:, 0:n], in_=pr[(g, kind)]["nrm_e"][:, 0:n])
+            pr[(g, kind)]["rinv"] = rinv
+
+        def finish(m):
+            g, b, i, nh = where(m)
+            o = ot[(g, b)]
+            if b < 2:
+                rinv = pr[(g, 0)]["rinv"]
+                rot = un[m]["rot"]
+                base = b * 8 + i * nh
+                for h in range(nh):
+                    nc.scalar.activation(out=o[:, h, i, :], in_=rot[:, h, :], func=ACT.Copy,
+                                         scale=rinv[:, base + h:base + h + 1])
+            if i == 1:
+                bt, a = divmod(g, 4)
+                ov = o[:].rearrange("p h i d -> p h (i d)")
+                if b < 2:
+                    nc.sync.dma_start(out=q_dst[bt][a][:, 4 * b:4 * (b + 1), :], in_=ov)
+                else:
+                    nc.sync.dma_start(out=k_dst[bt][a], in_=ov[:, 0:2, :])
+                    nc.sync.dma_start(out=v_dst[bt][a], in_=ov[:, 2:4, :])
+
+        def feed(m):
+            mx(m)
+            norms(m)
+
+        xs_of[0] = widen(0)
+        sines()
+        xg_of[0] = scaled(turn(xs_of[0]))
+        wg0 = wturn(0)
+        gains(0)
+        xq[0] = quant(xg_of[0])
+        wquant(0, wg0)
+        feed(0)
+        feed(1)
+        wquant(1, wturn(1))
+        feed(2)
+        feed(3)
+        root(0, 0)
+        xs_of[1] = widen(1)
+        xg_of[1] = scaled(turn(xs_of[1]))
+        gains(1)
+        gains(2)
+        gains(3)
+
+        for m in range(UNITS + LAG):
+            if m == 0:
+                wquant(2, wturn(2))
+            gm, r = divmod(m, 6)
+            for g in range(1, GROUPS):
+                if g > 1 and m == max(6 * g - 12, 1):
+                    tp_of[g] = turn(widen(g))
+                if m == 6 * g - 9:
+                    xg_of[g] = scaled(tp_of[g])
+                if m == max(6 * g - 6, 0):
+                    xq[g] = quant(xg_of[g])
+            if gm < GROUPS and r == 1:
+                invert(gm, 0)
+            if gm < GROUPS and r == 3:
+                invert(gm, 1)
+            if m + LEAD < UNITS:
+                feed(m + LEAD)
+            if gm < GROUPS and r == 0:
+                plus_eps(gm, 0)
+            if gm < GROUPS and r == 2:
+                plus_eps(gm, 1)
+            if m < UNITS:
+                rope_mul(m)
+                rope_add(m)
+            if m >= LAG:
+                finish(m - LAG)
+            if gm + 1 < GROUPS and r == 5:
+                root(gm + 1, 0)
+            if gm < GROUPS and r == 1:
+                root(gm, 1)

@@ -20,11 +20,13 @@ HALF = 64
 ROPE_BASE = 10000.0
 EPS = 1e-6
 GROUPS = 8
-BANKS = 3
-UNITS = 48
-LEAD = 4
-LAG = 3
+PAIRS = 24
 TWO_PI = 6.283185307179586
+LEAD = 2
+XCAST = 5
+XPROD = 4
+XQ = 3
+XG = 6
 
 FLOPS = 2 * 2048 * 1024 * 1536
 
@@ -47,12 +49,13 @@ def tile_gqaattention_pa_kernel(tc, x_bytes, x_scale, wq, wk, wv, gamma_q, gamma
 
         one = keep.tile([P, 1], F32, name="one")
         nc.vector.memset(one[:], 1.0)
-        first = keep.tile([P, 1], F32, name="first")
-        nc.scalar.activation(out=first[:], in_=one[:], func=ACT.Sin)
+        first = keep.tile([P, 2], F32, name="first")
+        nc.scalar.activation(out=first[:, 0:1], in_=one[:], func=ACT.Sin)
 
         xb = keep.tile([P, GROUPS, 2 * D], U8, name="x_bytes_sb")
         x_rows = x_bytes.rearrange("b t k -> (b t) k").rearrange("(g p i) k -> p g (i k)", p=P, i=2)
         scale_t = keep.tile([P, 2, 4], F32, name="scale_t")
+        scale_bc = keep.tile([P, D], F32, name="scale_bc")
         wraw = keep.tile([P, 12, D], BF16, name="wraw")
         gam_rows = keep.tile([P, 2 * HD], BF16, name="gam_rows")
         nc.vector.memset(gam_rows[:], 0.0)
@@ -62,18 +65,22 @@ def tile_gqaattention_pa_kernel(tc, x_bytes, x_scale, wq, wk, wv, gamma_q, gamma
         wq_rows = wq.rearrange("(a p) k -> p a k", p=P)
 
         nc.sync.dma_start(out=xb[:, 0:1, :], in_=x_rows[:, 0:1, :])
-        with nc.allow_non_contiguous_dma(reason="four scales to a partition and pass"):
-            nc.sync.dma_start(out=scale_t[:], in_=x_scale.rearrange("a b (c p t) -> p (a b c) t", p=P, t=4))
         nc.sync.dma_start(out=gam_rows[0:1, 0:HD], in_=gamma_q.unsqueeze(0))
         nc.sync.dma_start(out=gam_rows[0:1, HD:2 * HD], in_=gamma_k.unsqueeze(0))
-        nc.sync.dma_start(out=wraw[:, 0:2, :], in_=wq_rows[:, 0:2, :])
+        with nc.allow_non_contiguous_dma(reason="four scales to a partition and pass"):
+            nc.sync.dma_start(out=scale_t[:], in_=x_scale.rearrange("a b (c p t) -> p (a b c) t", p=P, t=4))
+        nc.sync.dma_start(out=wraw[:, 0:1, :], in_=wq_rows[:, 0:1, :])
+        nc.sync.dma_start(out=wraw[:, 1:2, :], in_=wq_rows[:, 1:2, :])
         nc.sync.dma_start(out=wraw[:, 2:4, :], in_=wq_rows[:, 2:4, :])
+        nc.sync.dma_start(out=wraw[:, 4:6, :], in_=wq_rows[:, 4:6, :])
+        nc.sync.dma_start(out=wraw[:, 6:8, :], in_=wq_rows[:, 6:8, :])
         nc.sync.dma_start(out=xb[:, 1:2, :], in_=x_rows[:, 1:2, :])
-        nc.sync.dma_start(out=wraw[:, 4:8, :], in_=wq_rows[:, 4:8, :])
         nc.sync.dma_start(out=wraw[:, 8:10, :], in_=wk.rearrange("(a p) k -> p a k", p=P))
         nc.sync.dma_start(out=wraw[:, 10:12, :], in_=wv.rearrange("(a p) k -> p a k", p=P))
         nc.sync.dma_start(out=xb[:, 2:4, :], in_=x_rows[:, 2:4, :])
         nc.sync.dma_start(out=xb[:, 4:8, :], in_=x_rows[:, 4:8, :])
+
+        nc.sync.dma_start(out=scale_bc[:], in_=x_scale.rearrange("a b k -> (a b k)").partition_broadcast(P))
 
         tpos = keep.tile([P, 8], F32, name="tpos")
         nc.gpsimd.iota(tpos[:], pattern=[[256, 4], [1, 2]], base=0, channel_multiplier=2,
@@ -85,7 +92,6 @@ def tile_gqaattention_pa_kernel(tc, x_bytes, x_scale, wq, wk, wv, gamma_q, gamma
         nc.tensor.matmul(out=gam_ps[:, 0].rearrange("p u r -> p (u r)"), lhsT=ones_sq[:], rhs=gam_rows[:], start=True, stop=True)
         nc.scalar.copy(out=gam[:].rearrange("p w d -> p (w d)"), in_=gam_ps[:, 0].rearrange("p u r -> p (u r)"))
 
-
         turns = keep.tile([P, 8], F32, name="turns")
         nc.vector.tensor_scalar(out=turns[:], in0=tpos[:], scalar1=1.0 / TWO_PI, scalar2=None, op0=ALU.mult)
         freq = keep.tile([P, HALF], F32, name="freq")
@@ -94,58 +100,64 @@ def tile_gqaattention_pa_kernel(tc, x_bytes, x_scale, wq, wk, wv, gamma_q, gamma
             nc.vector.tensor_scalar(out=freq[:, m:2 * m], in0=freq[:, 0:m], scalar1=ROPE_BASE ** (-m / HALF),
                                     scalar2=None, op0=ALU.mult)
         phi = keep.tile([P, 8, HALF], F32, name="phi")
-        nc.vector.tensor_tensor(out=phi[:], in0=turns[:].unsqueeze(2).to_broadcast([P, 8, HALF]),
-                                in1=freq[:].unsqueeze(1).to_broadcast([P, 8, HALF]), op=ALU.mult)
         whole_i = keep.tile([P, 8 * HALF], I32, name="whole_i")
-        phi_f = phi[:].rearrange("p a j -> p (a j)")
-        nc.vector.tensor_copy(out=whole_i[:], in_=phi_f)
         whole = keep.tile([P, 8 * HALF], F32, name="whole")
-        nc.vector.tensor_copy(out=whole[:], in_=whole_i[:])
         frac = keep.tile([P, 8 * HALF], F32, name="frac")
-        nc.vector.tensor_tensor(out=frac[:], in0=phi_f, in1=whole[:], op=ALU.subtract)
         negs = keep.tile([P, 8, HALF], F32, name="negs")
-        negs_f = negs[:].rearrange("p a j -> p (a j)")
-        nc.vector.scalar_tensor_tensor(out=negs_f, in0=frac[:], scalar=0.5, in1=frac[:], op0=ALU.is_gt,
-                                       op1=ALU.subtract)
         cq = keep.tile([P, 8 * HALF], F32, name="cq")
-        nc.vector.tensor_scalar(out=cq[:], in0=negs_f, scalar1=-1.0, scalar2=0.25, op0=ALU.mult, op1=ALU.add)
         negc = keep.tile([P, 8, HALF], F32, name="negc")
-        nc.vector.scalar_tensor_tensor(out=negc[:].rearrange("p a j -> p (a j)"), in0=cq[:], scalar=0.5, in1=cq[:],
-                                       op0=ALU.is_gt, op1=ALU.subtract)
         cos_t = keep.tile([P, 8, HALF], F32, name="cos_t")
         sin2 = keep.tile([P, 8, 2, HALF], F32, name="sin2")
-        rope = keep.tile([P, 2, 2, 8, HD], F32, name="rope")
 
-        def sines():
-            nc.scalar.activation(out=cos_t[:], in_=negc[:], func=ACT.Sin, scale=-TWO_PI)
-            nc.scalar.activation(out=sin2[:, :, 0, :], in_=negs[:], func=ACT.Sin, scale=TWO_PI)
-            nc.scalar.activation(out=sin2[:, :, 1, :], in_=negs[:], func=ACT.Sin, scale=-TWO_PI)
+        def angles(lo, hi):
+            cols = slice(HALF * lo, HALF * hi)
+            nc.vector.tensor_tensor(out=phi[:, lo:hi, :], in0=turns[:, lo:hi].unsqueeze(2).to_broadcast([P, hi - lo, HALF]),
+                                    in1=freq[:].unsqueeze(1).to_broadcast([P, hi - lo, HALF]), op=ALU.mult)
+            phi_f = phi[:].rearrange("p a j -> p (a j)")[:, cols]
+            nc.vector.tensor_copy(out=whole_i[:, cols], in_=phi_f)
+            nc.vector.tensor_copy(out=whole[:, cols], in_=whole_i[:, cols])
+            nc.vector.tensor_tensor(out=frac[:, cols], in0=phi_f, in1=whole[:, cols], op=ALU.subtract)
+            negs_f = negs[:].rearrange("p a j -> p (a j)")[:, cols]
+            nc.vector.scalar_tensor_tensor(out=negs_f, in0=frac[:, cols], scalar=0.5, in1=frac[:, cols], op0=ALU.is_gt,
+                                           op1=ALU.subtract)
+            nc.vector.tensor_scalar(out=cq[:, cols], in0=negs_f, scalar1=-1.0, scalar2=0.25, op0=ALU.mult, op1=ALU.add)
+            nc.vector.scalar_tensor_tensor(out=negc[:].rearrange("p a j -> p (a j)")[:, cols], in0=cq[:, cols], scalar=0.5,
+                                           in1=cq[:, cols], op0=ALU.is_gt, op1=ALU.subtract)
 
-        def gains(a):
-            gis = slice(2 * a, 2 * a + 2)
-            for w in range(2):
-                gv = gam[:, w, :].rearrange("p (s j) -> p s j", s=2).unsqueeze(1).to_broadcast([P, 2, 2, HALF])
-                nc.gpsimd.tensor_tensor(
-                    out=rope[:, w, 0, gis, :].rearrange("p a (s j) -> p a s j", s=2),
-                    in0=cos_t[:, gis, :].unsqueeze(2).to_broadcast([P, 2, 2, HALF]), in1=gv, op=ALU.mult)
-                nc.gpsimd.tensor_tensor(
-                    out=rope[:, w, 1, gis, :].rearrange("p a (s j) -> p a s j", s=2),
-                    in0=sin2[:, gis, :, :], in1=gv, op=ALU.mult)
+        def sines(lo, hi):
+            nc.scalar.activation(out=cos_t[:, lo:hi, :], in_=negc[:, lo:hi, :], func=ACT.Sin, scale=-TWO_PI)
+            nc.scalar.activation(out=sin2[:, lo:hi, 0, :], in_=negs[:, lo:hi, :], func=ACT.Sin, scale=TWO_PI)
+            nc.scalar.activation(out=sin2[:, lo:hi, 1, :], in_=negs[:, lo:hi, :], func=ACT.Sin, scale=-TWO_PI)
+
+        rope = keep.tile([P, 2, 8, 4, HALF], F32, name="rope")
+
+        def gains(lo, hi, w):
+            n = hi - lo
+            gv = gam[:, w, :].rearrange("p (s j) -> p s j", s=2).unsqueeze(1).to_broadcast([P, n, 2, HALF])
+            nc.gpsimd.tensor_tensor(out=rope[:, w, lo:hi, 0:4:3, :],
+                                    in0=cos_t[:, lo:hi, :].unsqueeze(2).to_broadcast([P, n, 2, HALF]), in1=gv, op=ALU.mult)
+            nc.gpsimd.tensor_tensor(out=rope[:, w, lo:hi, 1:3, :], in0=sin2[:, lo:hi, :, :], in1=gv, op=ALU.mult)
 
         wc = keep.tile([P, 2, 1536], U32, name="wc", align_bytes=64)
         wsc = keep.tile([P, 2, 1536], U8, name="wsc", align_bytes=64)
 
-        def turn_words(words, dst):
-            t = ring(banks, "tp", 2, [P, 2, 2, P], F32)
+        def turn_words(words, tp):
+            t = ring(banks, tp[0], tp[1], [P, 2, 2, P], F32)
             for c in range(2):
                 for u in range(2):
                     nc.tensor.transpose(t[:, c, u, :], words[:, 256 * c + u:256 * (c + 1):2], ident[:])
-            nc.scalar.copy(out=dst, in_=t[:].rearrange("p c u r -> p c r u"))
+            return t
 
-        def wturn(b):
+        def wturn(b, tp=("tp", 2), eng="SSSS"):
             wg = ring(rings, "wg", 2, [P, 2, 512, 2], F32, 64)
             for al in range(4):
-                turn_words(wraw[:, 4 * b + al, :].bitcast(F32), wg[:, :, P * al:P * (al + 1), :])
+                t = turn_words(wraw[:, 4 * b + al, :].bitcast(F32), tp)
+                dst = wg[:, :, P * al:P * (al + 1), :]
+                src = t[:].rearrange("p c u r -> p c r u")
+                if eng[al] == "S":
+                    nc.scalar.copy(out=dst, in_=src)
+                else:
+                    nc.vector.tensor_copy(out=dst, in_=src)
             return wg
 
         def wquant(b, wg):
@@ -154,27 +166,33 @@ def tile_gqaattention_pa_kernel(tc, x_bytes, x_scale, wq, wk, wv, gamma_q, gamma
                 nc.vector.quantize_mx(out=wc[:, c, cols].bitcast(FP8X4), scales=wsc[:, c, cols],
                                       in_=wg[:, c].rearrange("p f u -> p (f u)").bitcast(BF16))
 
+        def early(g, i):
+            return g >= 2 and i == 0
+
         def widen(g):
-            xs = ring(rings, "xs", 2, [P, 2, D], BF16)
+            xs = ring(rings, "xs", 3, [P, 2, D], BF16)
             for i in range(2):
                 nc.scalar.copy(out=xs[:, i, :], in_=xb[:, g, D * i:D * (i + 1)].bitcast(FP8))
-            return xs
-
-        def turn(xs):
-            ts = []
+            xw = {}
             for i in range(2):
-                words = xs[:, i, :].bitcast(F32)
-                t = ring(banks, "tp", 2, [P, 2, 2, P], F32)
-                for c in range(2):
-                    for u in range(2):
-                        nc.tensor.transpose(t[:, c, u, :], words[:, 256 * c + u:256 * (c + 1):2], ident[:])
-                ts.append(t)
-            return ts
+                if early(g, i):
+                    xw[i] = ring(rings, "xw", 2, [P, D], BF16)
+                    nc.gpsimd.tensor_tensor(out=xw[i][:], in0=xs[:, i, :], in1=scale_bc[:], op=ALU.mult)
+                else:
+                    xw[i] = xs[:, i, :]
+            return xw
 
-        def scaled(ts):
+        def turn(xw, tp=("tp", 2)):
+            return [turn_words(xw[i][:].bitcast(F32), tp) for i in range(2)]
+
+        def scaled(g, ts):
             xg = ring(rings, "xg", 2, [P, 2, 2, P, 4], BF16, 64)
             for i in range(2):
                 t = ts[i]
+                if early(g, i):
+                    nc.scalar.copy(out=xg[:, i].rearrange("p c r t -> p c (r t)").bitcast(F32).rearrange("p c (r u) -> p c r u", u=2),
+                                   in_=t[:].rearrange("p c u r -> p c r u"))
+                    continue
                 for c in range(2):
                     nc.vector.tensor_tensor(
                         out=xg[:, i, c].rearrange("p r (u e) -> p r u e", u=2),
@@ -193,176 +211,145 @@ def tile_gqaattention_pa_kernel(tc, x_bytes, x_scale, wq, wk, wv, gamma_q, gamma
         q_dst = [out_0[bt].rearrange("h (a p i) d -> a p h (i d)", a=4, p=P, i=2) for bt in range(2)]
         k_dst = [out_1[bt].rearrange("h (a p i) d -> a p h (i d)", a=4, p=P, i=2) for bt in range(2)]
         v_dst = [out_2[bt].rearrange("h (a p i) d -> a p h (i d)", a=4, p=P, i=2) for bt in range(2)]
-
-        xs_of = {}
-        xg_of = {}
-        tp_of = {}
         xq = {}
-        un = {}
-        pr = {}
-        ot = {}
+        acc_of = {}
+        ss_of = {}
+        nrm_of = {}
+        nrme_of = {}
+        rinv_of = {}
+        o_of = {}
+        pr_of = {}
 
-        def where(m):
-            g, r = divmod(m, 6)
-            b, i = divmod(r, 2)
-            return g, b, i, (4 if b < 2 else 2)
+        def where(j):
+            g, b = divmod(j, 3)
+            return g, b, (4 if b < 2 else 2)
 
-        def mx(m):
-            g, b, i, nh = where(m)
+        def mx(j):
+            g, b, nh = where(j)
             xc, xsc = xq[g]
-            acc = ring(banks, "acc", 6, [P, 512], F32)
-            for c in range(2):
-                lc = slice(256 * i + P * c, 256 * i + P * (c + 1))
-                rc = slice(512 * b, 512 * (b + 1))
-                nc.tensor.matmul_mx(out=acc[:], lhsT=xc[:, lc].bitcast(FP8X4), lhsT_scale=xsc[:, lc],
-                                    rhs=wc[:, c, rc].bitcast(FP8X4), rhs_scale=wsc[:, c, rc],
-                                    start=(c == 0), stop=(c == 1))
-            un[m] = {"acc": acc}
+            accs = []
+            for i in range(2):
+                acc = ring(banks, "acc", 6, [P, 512], F32)
+                for c in range(2):
+                    lc = slice(256 * i + P * c, 256 * i + P * (c + 1))
+                    rc = slice(512 * b, 512 * (b + 1))
+                    nc.tensor.matmul_mx(out=acc[:], lhsT=xc[:, lc].bitcast(FP8X4), lhsT_scale=xsc[:, lc],
+                                        rhs=wc[:, c, rc].bitcast(FP8X4), rhs_scale=wsc[:, c, rc],
+                                        start=(c == 0), stop=(c == 1))
+                accs.append(acc)
+            acc_of[j] = accs
 
-        def rope_mul(m):
-            g, b, i, nh = where(m)
-            gi = 2 * (g % 4) + i
-            acc = un[m]["acc"]
-            t1 = ring(rings, "ta", 4, [P, 4, HD], F32)
-            t2 = ring(rings, "tb", 4, [P, 4, HD], F32)
-            swapped = acc[:, 0:nh * HD].rearrange("p (h s j) -> p h s j", s=2, j=HALF)[:, :, ::-1, :]
-            if b < 2:
-                nc.vector.tensor_tensor(out=t1[:], in0=rope[:, 0, 0, gi, :].unsqueeze(1).to_broadcast([P, nh, HD]),
-                                        in1=acc[:].rearrange("p (h d) -> p h d", d=HD), op=ALU.mult)
-                nc.vector.tensor_tensor(
-                    out=t2[:].rearrange("p h (s j) -> p h s j", s=2),
-                    in0=rope[:, 0, 1, gi, :].rearrange("p (s j) -> p s j", s=2).unsqueeze(1).to_broadcast(
-                        [P, nh, 2, HALF]),
-                    in1=swapped, op=ALU.mult)
-            else:
-                rinv = pr[(g, 1)]["rinv"]
+        def squares(j):
+            g, b, nh = where(j)
+            ss = ring(rings, "ss", 4, [P, 8], F32)
+            for i in range(2):
+                acc = acc_of[j][i]
                 for h in range(nh):
-                    col = rinv[:, i * nh + h:i * nh + h + 1]
-                    nc.vector.scalar_tensor_tensor(out=t1[:, h, :], in0=acc[:, HD * h:HD * (h + 1)], scalar=col,
-                                                   in1=rope[:, 1, 0, gi, :], op0=ALU.mult, op1=ALU.mult)
-                    nc.vector.scalar_tensor_tensor(out=t2[:, h, :].rearrange("p (s j) -> p s j", s=2),
-                                                   in0=swapped[:, h], scalar=col,
-                                                   in1=rope[:, 1, 1, gi, :].rearrange("p (s j) -> p s j", s=2),
-                                                   op0=ALU.mult, op1=ALU.mult)
-            un[m]["t1"] = t1
-            un[m]["t2"] = t2
+                    junk = ring(rings, "junk", 4, [P, HD], BF16)
+                    nc.scalar.activation(out=junk[:], in_=acc[:, HD * h:HD * (h + 1)], func=ACT.Square,
+                                         accum_out=ss[:, i * nh + h:i * nh + h + 1])
+            ss_of[j] = ss
 
-        def rope_add(m):
-            g, b, i, nh = where(m)
-            if b < 2:
-                rot = ring(rings, "rot", 6, [P, nh, HD], F32)
-                un[m]["rot"] = rot
-                dst = rot[:]
-            else:
-                dst = ot[(g, b)][:, 0:2, i, :]
-            nc.gpsimd.tensor_tensor(out=dst, in0=un[m]["t1"][:, 0:nh], in1=un[m]["t2"][:, 0:nh], op=ALU.add)
-
-        def norms(m):
-            g, b, i, nh = where(m)
-            kind = 0 if b < 2 else 1
-            if i == 0:
-                o = ring(rings, "o", 6, [P, 4, 2, HD], F32)
-                ot[(g, b)] = o
-            if i == 0 and b != 1:
-                ss = ring(rings, "ss", 4, [P, 16], F32)
-                pr[(g, kind)] = {"ss": ss}
-            ss = pr[(g, kind)]["ss"]
-            acc = un[m]["acc"]
-            base = (b % 2) * 8 + i * nh
-            for h in range(nh):
-                junk = ring(rings, "junk", 4, [P, HD], BF16)
-                nc.scalar.activation(out=junk[:], in_=acc[:, HD * h:HD * (h + 1)], func=ACT.Square,
-                                     accum_out=ss[:, base + h:base + h + 1])
+        def vcopy(j):
+            g, b, nh = where(j)
             if b == 2:
-                nc.scalar.copy(out=ot[(g, b)][:, 2:4, i, :], in_=acc[:, 256:512].rearrange("p (h d) -> p h d", d=HD))
-
-        def root(g, kind):
-            n = 4 if kind else 16
-            nrm = ring(rings, "nrm", 4, [P, 16], F32)
-            nc.scalar.activation(out=nrm[:, 0:n], in_=pr[(g, kind)]["ss"][:, 0:n], func=ACT.Sqrt)
-            pr[(g, kind)]["nrm"] = nrm
-
-        def plus_eps(g, kind):
-            n = 4 if kind else 16
-            nrm_e = ring(rings, "nrme", 4, [P, 16], F32)
-            nc.scalar.activation(out=nrm_e[:, 0:n], in_=pr[(g, kind)]["nrm"][:, 0:n], func=ACT.Copy, bias=EPS)
-            pr[(g, kind)]["nrm_e"] = nrm_e
-
-        def invert(g, kind):
-            n = 4 if kind else 16
-            rinv = ring(rings, "rinv", 4, [P, 16], F32)
-            nc.vector.reciprocal(out=rinv[:, 0:n], in_=pr[(g, kind)]["nrm_e"][:, 0:n])
-            pr[(g, kind)]["rinv"] = rinv
-
-        def finish(m):
-            g, b, i, nh = where(m)
-            o = ot[(g, b)]
-            if b < 2:
-                rinv = pr[(g, 0)]["rinv"]
-                rot = un[m]["rot"]
-                base = b * 8 + i * nh
-                for h in range(nh):
-                    nc.scalar.activation(out=o[:, h, i, :], in_=rot[:, h, :], func=ACT.Copy,
-                                         scale=rinv[:, base + h:base + h + 1])
-            if i == 1:
+                ov = ring(rings, "ov", 2, [P, 2, 2, HD], F32)
+                for i in range(2):
+                    nc.scalar.copy(out=ov[:, :, i, :], in_=acc_of[j][i][:, 256:512].rearrange("p (h d) -> p h d", d=HD))
                 bt, a = divmod(g, 4)
-                ov = o[:].rearrange("p h i d -> p h (i d)")
-                if b < 2:
-                    nc.sync.dma_start(out=q_dst[bt][a][:, 4 * b:4 * (b + 1), :], in_=ov)
-                else:
-                    nc.sync.dma_start(out=k_dst[bt][a], in_=ov[:, 0:2, :])
-                    nc.sync.dma_start(out=v_dst[bt][a], in_=ov[:, 2:4, :])
+                nc.sync.dma_start(out=v_dst[bt][a], in_=ov[:].rearrange("p h i d -> p h (i d)"))
 
-        def feed(m):
-            mx(m)
-            norms(m)
+        def root(j):
+            n = 2 * where(j)[2]
+            nrm_of[j] = ring(rings, "nrm", 4, [P, 8], F32)
+            nc.scalar.activation(out=nrm_of[j][:, 0:n], in_=ss_of[j][:, 0:n], func=ACT.Sqrt)
 
-        xs_of[0] = widen(0)
-        sines()
-        xg_of[0] = scaled(turn(xs_of[0]))
-        wg0 = wturn(0)
-        gains(0)
-        xq[0] = quant(xg_of[0])
+        def plus_eps(j):
+            n = 2 * where(j)[2]
+            nrme_of[j] = ring(rings, "nrme", 4, [P, 8], F32)
+            nc.scalar.activation(out=nrme_of[j][:, 0:n], in_=nrm_of[j][:, 0:n], func=ACT.Copy, bias=EPS)
+
+        def invert(j):
+            n = 2 * where(j)[2]
+            rinv_of[j] = ring(rings, "rinv", 4, [P, 8], F32)
+            nc.vector.reciprocal(out=rinv_of[j][:, 0:n], in_=nrme_of[j][:, 0:n])
+
+        def products(j):
+            g, b, nh = where(j)
+            rinv = rinv_of[j]
+            pr = ring(rings, "pr", 3, [P, 4, 2, 4, HALF], F32)
+            for i in range(2):
+                gi = 2 * (g % 4) + i
+                acc = acc_of[j][i]
+                for h in range(nh):
+                    nc.vector.scalar_tensor_tensor(
+                        out=pr[:, h, i].rearrange("p (d s) j -> p d (s j)", d=2),
+                        in0=acc[:, HD * h:HD * (h + 1)].unsqueeze(1).to_broadcast([P, 2, HD]),
+                        scalar=rinv[:, i * nh + h:i * nh + h + 1],
+                        in1=rope[:, b // 2, gi].rearrange("p (d s) j -> p d (s j)", d=2),
+                        op0=ALU.mult, op1=ALU.mult)
+            pr_of[j] = pr
+
+        def adds(j):
+            g, b, nh = where(j)
+            o = ring(rings, "o", 4, [P, 4, 2, HD], F32)
+            pv = pr_of[j][:, 0:nh].rearrange("p h i (d s) j -> p (h i d) s j", s=2)
+            nc.gpsimd.tensor_tensor(out=o[:, 0:nh].rearrange("p h i (d j) -> p (h i d) j", d=2),
+                                    in0=pv[:, :, 0, :], in1=pv[:, :, 1, :], op=ALU.add)
+            bt, a = divmod(g, 4)
+            ov = o[:].rearrange("p h i d -> p h (i d)")
+            if b < 2:
+                nc.sync.dma_start(out=q_dst[bt][a][:, 4 * b:4 * (b + 1), :], in_=ov)
+            else:
+                nc.sync.dma_start(out=k_dst[bt][a], in_=ov[:, 0:2, :])
+
+        angles(0, 2)
+        sines(0, 2)
+        xs0 = widen(0)
+        angles(2, 8)
+        sines(2, 8)
+        nc.scalar.activation(out=first[:, 1:2], in_=sin2[:, 7, 1, 0:1], func=ACT.Sqrt, scale=0.0, bias=1.0)
+        wg0 = wturn(0, ("acc", 6), "SVVV")
+        xg0 = scaled(0, turn(xs0))
+        gains(0, 2, 0)
+        xq[0] = quant(xg0)
         wquant(0, wg0)
-        feed(0)
-        feed(1)
-        wquant(1, wturn(1))
-        feed(2)
-        feed(3)
-        root(0, 0)
-        xs_of[1] = widen(1)
-        xg_of[1] = scaled(turn(xs_of[1]))
-        gains(1)
-        gains(2)
-        gains(3)
+        mx(0)
+        squares(0)
+        root(0)
+        plus_eps(0)
+        invert(0)
+        wquant(1, wturn(1, ("acc", 6), "SVSV"))
+        gains(0, 2, 1)
+        tp_of = {}
+        xw_of = {}
+        xg_of = {}
 
-        for m in range(UNITS + LAG):
-            if m == 0:
+        for j in range(PAIRS):
+            if j == 0:
+                mx(1)
+                squares(1)
+            if j >= 0:
+                products(j)
+                adds(j)
+            if j == 0:
                 wquant(2, wturn(2))
-            gm, r = divmod(m, 6)
+                for w in range(2):
+                    gains(2, 8, w)
+            if j + 1 < PAIRS:
+                root(j + 1)
+                plus_eps(j + 1)
+                invert(j + 1)
+            if j + 2 < PAIRS:
+                mx(j + 2)
+                squares(j + 2)
+                vcopy(j + 2)
             for g in range(1, GROUPS):
-                if g > 1 and m == max(6 * g - 12, 1):
-                    tp_of[g] = turn(widen(g))
-                if m == 6 * g - 9:
-                    xg_of[g] = scaled(tp_of[g])
-                if m == max(6 * g - 6, 0):
+                if j == max(3 * g - XG, 0):
+                    xw_of[g] = widen(g)
+                if j == max(3 * g - XCAST, 0):
+                    tp_of[g] = turn(xw_of[g])
+                if j == max(3 * g - XPROD, 0):
+                    xg_of[g] = scaled(g, tp_of[g])
+                if j == max(3 * g - XQ, 0):
                     xq[g] = quant(xg_of[g])
-            if gm < GROUPS and r == 1:
-                invert(gm, 0)
-            if gm < GROUPS and r == 3:
-                invert(gm, 1)
-            if m + LEAD < UNITS:
-                feed(m + LEAD)
-            if gm < GROUPS and r == 0:
-                plus_eps(gm, 0)
-            if gm < GROUPS and r == 2:
-                plus_eps(gm, 1)
-            if m < UNITS:
-                rope_mul(m)
-                rope_add(m)
-            if m >= LAG:
-                finish(m - LAG)
-            if gm + 1 < GROUPS and r == 5:
-                root(gm + 1, 0)
-            if gm < GROUPS and r == 1:
-                root(gm, 1)

@@ -27,6 +27,8 @@ XCAST = 5
 XPROD = 4
 XQ = 3
 XG = 6
+SPLIT = 2
+XO = -3
 
 FLOPS = 2 * 2048 * 1024 * 1536
 
@@ -37,6 +39,7 @@ def tile_gqaattention_pa_kernel(tc, x_bytes, x_scale, wq, wk, wv, gamma_q, gamma
         keep = ctx.enter_context(tc.tile_pool(name="keep", bufs=1))
         rings = ctx.enter_context(tc.tile_pool(name="rings", bufs=1))
         banks = ctx.enter_context(tc.psum_pool(name="banks", bufs=1))
+        ctx.enter_context(tc.manual_schedule())
         taken = {}
 
         def ring(pool, base, depth, shape, dtype, align=None):
@@ -90,7 +93,10 @@ def tile_gqaattention_pa_kernel(tc, x_bytes, x_scale, wq, wk, wv, gamma_q, gamma
 
         gam_ps = ring(banks, "tp", 2, [P, 2, 2, P], F32)
         nc.tensor.matmul(out=gam_ps[:, 0].rearrange("p u r -> p (u r)"), lhsT=ones_sq[:], rhs=gam_rows[:], start=True, stop=True)
-        nc.scalar.copy(out=gam[:].rearrange("p w d -> p (w d)"), in_=gam_ps[:, 0].rearrange("p u r -> p (u r)"))
+
+        def gam_copy():
+            nc.scalar.copy(out=gam[:].rearrange("p w d -> p (w d)"), in_=gam_ps[:, 0].rearrange("p u r -> p (u r)"))
+
 
         turns = keep.tile([P, 8], F32, name="turns")
         nc.vector.tensor_scalar(out=turns[:], in0=tpos[:], scalar1=1.0 / TWO_PI, scalar2=None, op0=ALU.mult)
@@ -148,58 +154,65 @@ def tile_gqaattention_pa_kernel(tc, x_bytes, x_scale, wq, wk, wv, gamma_q, gamma
                     nc.tensor.transpose(t[:, c, u, :], words[:, 256 * c + u:256 * (c + 1):2], ident[:])
             return t
 
-        def wturn(b, tp=("tp", 2), eng="SSSS"):
-            wg = ring(rings, "wg", 2, [P, 2, 512, 2], F32, 64)
-            for al in range(4):
-                t = turn_words(wraw[:, 4 * b + al, :].bitcast(F32), tp)
-                dst = wg[:, :, P * al:P * (al + 1), :]
-                src = t[:].rearrange("p c u r -> p c r u")
-                if eng[al] == "S":
-                    nc.scalar.copy(out=dst, in_=src)
-                else:
-                    nc.vector.tensor_copy(out=dst, in_=src)
-            return wg
+        wg_of = {}
+        wt_of = {}
 
-        def wquant(b, wg):
+        def wturn(n, tp=("acc", 6)):
+            wt_of[n] = turn_words(wraw[:, n, :].bitcast(F32), tp)
+
+        def wcopy(n, eng):
+            b, al = divmod(n, 4)
+            if al == 0:
+                wg_of[b] = ring(rings, "wg", 2, [P, 2, 512, 2], F32, 64)
+            dst = wg_of[b][:, :, P * al:P * (al + 1), :]
+            src = wt_of[n][:].rearrange("p c u r -> p c r u")
+            if eng == "S":
+                nc.scalar.copy(out=dst, in_=src)
+            else:
+                nc.vector.tensor_copy(out=dst, in_=src)
+
+        def wquant(b):
+            wg = wg_of[b]
             for c in range(2):
                 cols = slice(512 * b, 512 * (b + 1))
                 nc.vector.quantize_mx(out=wc[:, c, cols].bitcast(FP8X4), scales=wsc[:, c, cols],
                                       in_=wg[:, c].rearrange("p f u -> p (f u)").bitcast(BF16))
 
         def early(g, i):
-            return g >= 2 and i == 0
+            return False
 
-        def widen(g):
-            xs = ring(rings, "xs", 3, [P, 2, D], BF16)
-            for i in range(2):
-                nc.scalar.copy(out=xs[:, i, :], in_=xb[:, g, D * i:D * (i + 1)].bitcast(FP8))
-            xw = {}
-            for i in range(2):
-                if early(g, i):
-                    xw[i] = ring(rings, "xw", 2, [P, D], BF16)
-                    nc.gpsimd.tensor_tensor(out=xw[i][:], in0=xs[:, i, :], in1=scale_bc[:], op=ALU.mult)
-                else:
-                    xw[i] = xs[:, i, :]
-            return xw
+        xs_of = {}
+        xt_of = {}
+        xg_of = {}
 
-        def turn(xw, tp=("tp", 2)):
-            return [turn_words(xw[i][:].bitcast(F32), tp) for i in range(2)]
+        def cast(g, i):
+            xs_of[g, i] = ring(rings, "xs", 4, [P, D], BF16)
+            nc.scalar.copy(out=xs_of[g, i][:], in_=xb[:, g, D * i:D * (i + 1)].bitcast(FP8))
 
-        def scaled(g, ts):
-            xg = ring(rings, "xg", 2, [P, 2, 2, P, 4], BF16, 64)
-            for i in range(2):
-                t = ts[i]
-                if early(g, i):
-                    nc.scalar.copy(out=xg[:, i].rearrange("p c r t -> p c (r t)").bitcast(F32).rearrange("p c (r u) -> p c r u", u=2),
-                                   in_=t[:].rearrange("p c u r -> p c r u"))
-                    continue
+        def prescale(g, i):
+            if early(g, i):
+                xw = ring(rings, "xw", 2, [P, D], BF16)
+                nc.gpsimd.tensor_tensor(out=xw[:], in0=xs_of[g, i][:], in1=scale_bc[:], op=ALU.mult)
+                xs_of[g, i] = xw
+
+        def turn(g, i, tp=("tp", 2)):
+            xt_of[g, i] = turn_words(xs_of[g, i][:].bitcast(F32), tp)
+
+        def gather(g, i):
+            if g not in xg_of:
+                xg_of[g] = ring(rings, "xg", 2, [P, 2, 2, P, 4], BF16, 64)
+            xg = xg_of[g]
+            t = xt_of[g, i]
+            if early(g, i):
+                nc.scalar.copy(out=xg[:, i].rearrange("p c r t -> p c (r t)").bitcast(F32).rearrange("p c (r u) -> p c r u", u=2),
+                               in_=t[:].rearrange("p c u r -> p c r u"))
+            else:
                 for c in range(2):
                     nc.vector.tensor_tensor(
                         out=xg[:, i, c].rearrange("p r (u e) -> p r u e", u=2),
                         in0=scale_t[:, c, :].rearrange("p (u e) -> p u e", u=2).unsqueeze(1).to_broadcast([P, P, 2, 2]),
                         in1=t[:, c].rearrange("p u r -> p (u r)").bitcast(BF16).rearrange("p (u r e) -> p r u e", u=2, e=2),
                         op=ALU.mult)
-            return xg
 
         def quant(xg):
             xc = ring(rings, "xc", 4, [P, 512], U32, 64)
@@ -219,45 +232,41 @@ def tile_gqaattention_pa_kernel(tc, x_bytes, x_scale, wq, wk, wv, gamma_q, gamma
         rinv_of = {}
         o_of = {}
         pr_of = {}
+        r_of = {}
+        ov_of = {}
 
         def where(j):
             g, b = divmod(j, 3)
             return g, b, (4 if b < 2 else 2)
 
-        def mx(j):
+        def mx(j, i):
             g, b, nh = where(j)
             xc, xsc = xq[g]
-            accs = []
-            for i in range(2):
-                acc = ring(banks, "acc", 6, [P, 512], F32)
-                for c in range(2):
-                    lc = slice(256 * i + P * c, 256 * i + P * (c + 1))
-                    rc = slice(512 * b, 512 * (b + 1))
-                    nc.tensor.matmul_mx(out=acc[:], lhsT=xc[:, lc].bitcast(FP8X4), lhsT_scale=xsc[:, lc],
-                                        rhs=wc[:, c, rc].bitcast(FP8X4), rhs_scale=wsc[:, c, rc],
-                                        start=(c == 0), stop=(c == 1))
-                accs.append(acc)
-            acc_of[j] = accs
+            acc = ring(banks, "acc", 6, [P, 512], F32)
+            for c in range(2):
+                lc = slice(256 * i + P * c, 256 * i + P * (c + 1))
+                rc = slice(512 * b, 512 * (b + 1))
+                nc.tensor.matmul_mx(out=acc[:], lhsT=xc[:, lc].bitcast(FP8X4), lhsT_scale=xsc[:, lc],
+                                    rhs=wc[:, c, rc].bitcast(FP8X4), rhs_scale=wsc[:, c, rc],
+                                    start=(c == 0), stop=(c == 1))
+            acc_of[j, i] = acc
 
-        def squares(j):
+        def squares(j, i):
             g, b, nh = where(j)
-            ss = ring(rings, "ss", 4, [P, 8], F32)
-            for i in range(2):
-                acc = acc_of[j][i]
-                for h in range(nh):
-                    junk = ring(rings, "junk", 4, [P, HD], BF16)
-                    nc.scalar.activation(out=junk[:], in_=acc[:, HD * h:HD * (h + 1)], func=ACT.Square,
-                                         accum_out=ss[:, i * nh + h:i * nh + h + 1])
-            ss_of[j] = ss
+            if i == 0:
+                ss_of[j] = ring(rings, "ss", 4, [P, 8], F32)
+            for h in range(nh):
+                junk = ring(rings, "junk", 4, [P, HD], BF16)
+                nc.scalar.activation(out=junk[:], in_=acc_of[j, i][:, HD * h:HD * (h + 1)], func=ACT.Square,
+                                     accum_out=ss_of[j][:, i * nh + h:i * nh + h + 1])
 
         def vcopy(j):
             g, b, nh = where(j)
             if b == 2:
                 ov = ring(rings, "ov", 2, [P, 2, 2, HD], F32)
                 for i in range(2):
-                    nc.scalar.copy(out=ov[:, :, i, :], in_=acc_of[j][i][:, 256:512].rearrange("p (h d) -> p h d", d=HD))
-                bt, a = divmod(g, 4)
-                nc.sync.dma_start(out=v_dst[bt][a], in_=ov[:].rearrange("p h i d -> p h (i d)"))
+                    nc.scalar.copy(out=ov[:, :, i, :], in_=acc_of[j, i][:, 256:512].rearrange("p (h d) -> p h d", d=HD))
+                ov_of[j] = ov
 
         def root(j):
             n = 2 * where(j)[2]
@@ -274,28 +283,59 @@ def tile_gqaattention_pa_kernel(tc, x_bytes, x_scale, wq, wk, wv, gamma_q, gamma
             rinv_of[j] = ring(rings, "rinv", 4, [P, 8], F32)
             nc.vector.reciprocal(out=rinv_of[j][:, 0:n], in_=nrme_of[j][:, 0:n])
 
-        def products(j):
-            g, b, nh = where(j)
-            rinv = rinv_of[j]
-            pr = ring(rings, "pr", 3, [P, 4, 2, 4, HALF], F32)
-            for i in range(2):
-                gi = 2 * (g % 4) + i
-                acc = acc_of[j][i]
-                for h in range(nh):
-                    nc.vector.scalar_tensor_tensor(
-                        out=pr[:, h, i].rearrange("p (d s) j -> p d (s j)", d=2),
-                        in0=acc[:, HD * h:HD * (h + 1)].unsqueeze(1).to_broadcast([P, 2, HD]),
-                        scalar=rinv[:, i * nh + h:i * nh + h + 1],
-                        in1=rope[:, b // 2, gi].rearrange("p (d s) j -> p d (s j)", d=2),
-                        op0=ALU.mult, op1=ALU.mult)
-            pr_of[j] = pr
+        def folded(j):
+            return j > 0
 
-        def adds(j):
+        def products(j, i):
             g, b, nh = where(j)
-            o = ring(rings, "o", 4, [P, 4, 2, HD], F32)
-            pv = pr_of[j][:, 0:nh].rearrange("p h i (d s) j -> p (h i d) s j", s=2)
-            nc.gpsimd.tensor_tensor(out=o[:, 0:nh].rearrange("p h i (d j) -> p (h i d) j", d=2),
-                                    in0=pv[:, :, 0, :], in1=pv[:, :, 1, :], op=ALU.add)
+            if i == 0:
+                pr_of[j] = ring(rings, "pr", 3, [P, 4, 2, 4, HALF], F32)
+            pr = pr_of[j]
+            if True:
+                gi = 2 * (g % 4) + i
+                acc = acc_of[j, i]
+                table = rope[:, b // 2, gi].rearrange("p (d s) j -> p d (s j)", d=2)
+                if folded(j):
+                    for h in range(nh):
+                        nc.vector.scalar_tensor_tensor(
+                            out=pr[:, h, i].rearrange("p (d s) j -> p d (s j)", d=2),
+                            in0=acc[:, HD * h:HD * (h + 1)].unsqueeze(1).to_broadcast([P, 2, HD]),
+                            scalar=rinv_of[j][:, i * nh + h:i * nh + h + 1], in1=table, op0=ALU.mult, op1=ALU.mult)
+                else:
+                    nc.vector.tensor_tensor(
+                        out=pr[:, 0:nh, i].rearrange("p h (d s) j -> p h d (s j)", d=2),
+                        in0=table.unsqueeze(1).to_broadcast([P, nh, 2, HD]),
+                        in1=acc[:, 0:nh * HD].rearrange("p (h d) -> p h d", d=HD).unsqueeze(2).to_broadcast([P, nh, 2, HD]),
+                        op=ALU.mult)
+
+        def adds(j, i):
+            g, b, nh = where(j)
+            if i == 0:
+                o_of[j] = ring(rings, "o", 5, [P, 4, 2, HD], F32)
+                if not folded(j):
+                    r_of[j] = ring(rings, "r", 3, [P, 4, 2, HD], F32)
+            r = o_of[j] if folded(j) else r_of[j]
+            pv = pr_of[j][:, 0:nh, i].rearrange("p h (d s) j -> p h d s j", s=2)
+            eng = nc.vector if j == PAIRS - 1 else nc.gpsimd
+            eng.tensor_tensor(out=r[:, 0:nh, i, :].rearrange("p h (d j) -> p h d j", d=2),
+                              in0=pv[:, :, :, 0, :], in1=pv[:, :, :, 1, :], op=ALU.add)
+
+        def scalings(j):
+            if not folded(j):
+                for h in range(4):
+                    for i in range(2):
+                        nc.scalar.activation(out=o_of[j][:, h, i, :], in_=r_of[j][:, h, i, :], func=ACT.Copy,
+                                             scale=rinv_of[j][:, i * 4 + h:i * 4 + h + 1])
+
+        def vstore(j):
+            g, b, nh = where(j)
+            if b == 2:
+                bt, a = divmod(g, 4)
+                nc.sync.dma_start(out=v_dst[bt][a], in_=ov_of[j][:].rearrange("p h i d -> p h (i d)"))
+
+        def store(j):
+            g, b, nh = where(j)
+            o = o_of[j]
             bt, a = divmod(g, 4)
             ov = o[:].rearrange("p h i d -> p h (i d)")
             if b < 2:
@@ -303,53 +343,141 @@ def tile_gqaattention_pa_kernel(tc, x_bytes, x_scale, wq, wk, wv, gamma_q, gamma
             else:
                 nc.sync.dma_start(out=k_dst[bt][a], in_=ov[:, 0:2, :])
 
+        def xwork(j, slot):
+            for g in range(2, GROUPS):
+                for what, when in XPLAN[early(g, 0)]:
+                    if when == 4 * (j - 3 * g) + slot:
+                        what(g)
+
+        XPLAN = {
+            True: ((lambda g: cast(g, 0), -34), (lambda g: prescale(g, 0), -31), (lambda g: cast(g, 1), -26), (lambda g: turn(g, 1), -21),
+                   (lambda g: gather(g, 1), -17), (lambda g: turn(g, 0), -17), (lambda g: gather(g, 0), -15), (lambda g: xquant(g), -13)),
+            False: ((lambda g: cast(g, 0), -30), (lambda g: cast(g, 1), -26), (lambda g: turn(g, 0), -25), (lambda g: gather(g, 0), -21), (lambda g: turn(g, 1), -21),
+                    (lambda g: gather(g, 1), -17), (lambda g: xquant(g), -13)),
+        }
+
+        def xquant(g):
+            xq[g] = quant(xg_of[g])
+
         angles(0, 2)
+        cast(0, 0)
+        gam_copy()
         sines(0, 2)
-        xs0 = widen(0)
-        angles(2, 8)
-        sines(2, 8)
-        nc.scalar.activation(out=first[:, 1:2], in_=sin2[:, 7, 1, 0:1], func=ACT.Sqrt, scale=0.0, bias=1.0)
-        wg0 = wturn(0, ("acc", 6), "SVVV")
-        xg0 = scaled(0, turn(xs0))
+        cast(0, 1)
         gains(0, 2, 0)
-        xq[0] = quant(xg0)
-        wquant(0, wg0)
-        mx(0)
-        squares(0)
+        gains(0, 2, 1)
+        angles(2, 8)
+        wturn(0)
+        wturn(1)
+        turn(0, 0)
+        wturn(2)
+        turn(0, 1)
+        wturn(3)
+        wcopy(0, "V")
+        wcopy(1, "S")
+        gather(0, 0)
+        wcopy(2, "S")
+        gather(0, 1)
+        wcopy(3, "S")
+        sines(2, 8)
+        gains(2, 8, 0)
+        xq[0] = quant(xg_of[0])
+        wquant(0)
+        for n in range(4, 8):
+            wturn(n)
+        mx(0, 0)
+        mx(0, 1)
+        wcopy(4, "S")
+        wcopy(5, "S")
+        wcopy(6, "V")
+        wcopy(7, "S")
+        cast(1, 0)
+        wturn(8)
+        wturn(9)
+        turn(1, 0)
+        wquant(1)
+        squares(0, 0)
+        squares(0, 1)
+        mx(1, 0)
+        mx(1, 1)
+        products(0, 0)
+        adds(0, 0)
+        products(0, 1)
+        adds(0, 1)
+        wcopy(8, "S")
+        wcopy(9, "S")
+        cast(1, 1)
+        gather(1, 0)
+        turn(1, 1)
+        squares(1, 0)
+        squares(1, 1)
+        nc.scalar.activation(out=first[:, 1:2], in_=sin2[:, 7, 1, 0:1], func=ACT.Sqrt, scale=0.0, bias=1.0)
+        root(1)
+        plus_eps(1)
+        wturn(10)
+        wturn(11)
+        gather(1, 1)
+        xq[1] = quant(xg_of[1])
+        invert(1)
+        products(1, 0)
+        adds(1, 0)
+        wcopy(10, "V")
+        wcopy(11, "S")
+        wquant(2)
+        products(1, 1)
+        adds(1, 1)
+        gains(2, 8, 1)
+        for s in range(-16, 4):
+            xwork(s // 4, s % 4)
+        mx(2, 0)
+        mx(2, 1)
+        squares(2, 0)
+        squares(2, 1)
+        root(2)
+        vcopy(2)
+        plus_eps(2)
         root(0)
         plus_eps(0)
+        vstore(2)
+        for s in range(4, 8):
+            xwork(s // 4, s % 4)
+        invert(2)
         invert(0)
-        wquant(1, wturn(1, ("acc", 6), "SVSV"))
-        gains(0, 2, 1)
-        tp_of = {}
-        xw_of = {}
-        xg_of = {}
+        scalings(0)
+        store(0)
+        store(1)
+        mx(3, 0)
+        mx(3, 1)
+        squares(3, 0)
+        squares(3, 1)
+        root(3)
+        plus_eps(3)
+        mx(4, 0)
 
-        for j in range(PAIRS):
-            if j == 0:
-                mx(1)
-                squares(1)
-            if j >= 0:
-                products(j)
-                adds(j)
-            if j == 0:
-                wquant(2, wturn(2))
-                for w in range(2):
-                    gains(2, 8, w)
-            if j + 1 < PAIRS:
-                root(j + 1)
-                plus_eps(j + 1)
-                invert(j + 1)
+        for j in range(2, PAIRS + 1):
             if j + 2 < PAIRS:
-                mx(j + 2)
-                squares(j + 2)
+                mx(j + 2, 1)
+                squares(j + 2, 0)
+            xwork(j, 0)
+            if j < PAIRS:
+                products(j, 0)
+                adds(j, 0)
+            xwork(j, 1)
+            if j + 3 < PAIRS:
+                mx(j + 3, 0)
+            if j + 2 < PAIRS:
+                squares(j + 2, 1)
+                root(j + 2)
                 vcopy(j + 2)
-            for g in range(1, GROUPS):
-                if j == max(3 * g - XG, 0):
-                    xw_of[g] = widen(g)
-                if j == max(3 * g - XCAST, 0):
-                    tp_of[g] = turn(xw_of[g])
-                if j == max(3 * g - XPROD, 0):
-                    xg_of[g] = scaled(g, tp_of[g])
-                if j == max(3 * g - XQ, 0):
-                    xq[g] = quant(xg_of[g])
+            xwork(j, 2)
+            if j + 2 < PAIRS:
+                plus_eps(j + 2)
+                vstore(j + 2)
+            if j + 1 < PAIRS:
+                invert(j + 1)
+            if j < PAIRS:
+                products(j, 1)
+                adds(j, 1)
+            xwork(j, 3)
+            if j > 2:
+                store(j - 1)

@@ -75,9 +75,9 @@ def tile_gqaattention_pa_kernel(tc, x_bytes, x_scale, wq, wk, wv, gamma_q, gamma
         nc.sync.dma_start(out=wraw[:, 0:1, :], in_=wq_rows[:, 0:1, :])
         nc.sync.dma_start(out=wraw[:, 1:2, :], in_=wq_rows[:, 1:2, :])
         nc.sync.dma_start(out=wraw[:, 2:4, :], in_=wq_rows[:, 2:4, :])
+        nc.sync.dma_start(out=xb[:, 1:2, :], in_=x_rows[:, 1:2, :])
         nc.sync.dma_start(out=wraw[:, 4:6, :], in_=wq_rows[:, 4:6, :])
         nc.sync.dma_start(out=wraw[:, 6:8, :], in_=wq_rows[:, 6:8, :])
-        nc.sync.dma_start(out=xb[:, 1:2, :], in_=x_rows[:, 1:2, :])
         nc.sync.dma_start(out=wraw[:, 8:10, :], in_=wk.rearrange("(a p) k -> p a k", p=P))
         nc.sync.dma_start(out=wraw[:, 10:12, :], in_=wv.rearrange("(a p) k -> p a k", p=P))
         nc.sync.dma_start(out=xb[:, 2:4, :], in_=x_rows[:, 2:4, :])
@@ -91,7 +91,7 @@ def tile_gqaattention_pa_kernel(tc, x_bytes, x_scale, wq, wk, wv, gamma_q, gamma
         ident = keep.tile([P, P], F32, name="ident")
         make_identity(nc, ident[:])
 
-        gam_ps = ring(banks, "tp", 2, [P, 2, 2, P], F32)
+        gam_ps = ring(banks, "tp", 1, [P, 2, 2, P], F32)
         nc.tensor.matmul(out=gam_ps[:, 0].rearrange("p u r -> p (u r)"), lhsT=ones_sq[:], rhs=gam_rows[:], start=True, stop=True)
 
         def gam_copy():
@@ -115,20 +115,26 @@ def tile_gqaattention_pa_kernel(tc, x_bytes, x_scale, wq, wk, wv, gamma_q, gamma
         cos_t = keep.tile([P, 8, HALF], F32, name="cos_t")
         sin2 = keep.tile([P, 8, 2, HALF], F32, name="sin2")
 
-        def angles(lo, hi):
-            cols = slice(HALF * lo, HALF * hi)
-            nc.vector.tensor_tensor(out=phi[:, lo:hi, :], in0=turns[:, lo:hi].unsqueeze(2).to_broadcast([P, hi - lo, HALF]),
-                                    in1=freq[:].unsqueeze(1).to_broadcast([P, hi - lo, HALF]), op=ALU.mult)
-            phi_f = phi[:].rearrange("p a j -> p (a j)")[:, cols]
-            nc.vector.tensor_copy(out=whole_i[:, cols], in_=phi_f)
-            nc.vector.tensor_copy(out=whole[:, cols], in_=whole_i[:, cols])
-            nc.vector.tensor_tensor(out=frac[:, cols], in0=phi_f, in1=whole[:, cols], op=ALU.subtract)
-            negs_f = negs[:].rearrange("p a j -> p (a j)")[:, cols]
-            nc.vector.scalar_tensor_tensor(out=negs_f, in0=frac[:, cols], scalar=0.5, in1=frac[:, cols], op0=ALU.is_gt,
-                                           op1=ALU.subtract)
-            nc.vector.tensor_scalar(out=cq[:, cols], in0=negs_f, scalar1=-1.0, scalar2=0.25, op0=ALU.mult, op1=ALU.add)
-            nc.vector.scalar_tensor_tensor(out=negc[:].rearrange("p a j -> p (a j)")[:, cols], in0=cq[:, cols], scalar=0.5,
-                                           in1=cq[:, cols], op0=ALU.is_gt, op1=ALU.subtract)
+        def angles(spans):
+            def each(f):
+                for lo, hi in spans:
+                    f(lo, hi, slice(HALF * lo, HALF * hi))
+
+            phi_f = phi[:].rearrange("p a j -> p (a j)")
+            negs_f = negs[:].rearrange("p a j -> p (a j)")
+            negc_f = negc[:].rearrange("p a j -> p (a j)")
+            each(lambda lo, hi, c: nc.vector.tensor_tensor(
+                out=phi[:, lo:hi, :], in0=turns[:, lo:hi].unsqueeze(2).to_broadcast([P, hi - lo, HALF]),
+                in1=freq[:].unsqueeze(1).to_broadcast([P, hi - lo, HALF]), op=ALU.mult))
+            each(lambda lo, hi, c: nc.vector.tensor_copy(out=whole_i[:, c], in_=phi_f[:, c]))
+            each(lambda lo, hi, c: nc.vector.tensor_copy(out=whole[:, c], in_=whole_i[:, c]))
+            each(lambda lo, hi, c: nc.vector.tensor_tensor(out=frac[:, c], in0=phi_f[:, c], in1=whole[:, c], op=ALU.subtract))
+            each(lambda lo, hi, c: nc.vector.scalar_tensor_tensor(out=negs_f[:, c], in0=frac[:, c], scalar=0.5, in1=frac[:, c],
+                                                                  op0=ALU.is_gt, op1=ALU.subtract))
+            each(lambda lo, hi, c: nc.vector.tensor_scalar(out=cq[:, c], in0=negs_f[:, c], scalar1=-1.0, scalar2=0.25,
+                                                           op0=ALU.mult, op1=ALU.add))
+            each(lambda lo, hi, c: nc.vector.scalar_tensor_tensor(out=negc_f[:, c], in0=cq[:, c], scalar=0.5, in1=cq[:, c],
+                                                                  op0=ALU.is_gt, op1=ALU.subtract))
 
         def sines(lo, hi):
             nc.scalar.activation(out=cos_t[:, lo:hi, :], in_=negc[:, lo:hi, :], func=ACT.Sin, scale=-TWO_PI)
@@ -157,7 +163,7 @@ def tile_gqaattention_pa_kernel(tc, x_bytes, x_scale, wq, wk, wv, gamma_q, gamma
         wg_of = {}
         wt_of = {}
 
-        def wturn(n, tp=("acc", 6)):
+        def wturn(n, tp=("acc", 7)):
             wt_of[n] = turn_words(wraw[:, n, :].bitcast(F32), tp)
 
         def wcopy(n, eng):
@@ -187,7 +193,10 @@ def tile_gqaattention_pa_kernel(tc, x_bytes, x_scale, wq, wk, wv, gamma_q, gamma
 
         def cast(g, i):
             xs_of[g, i] = ring(rings, "xs", 4, [P, D], BF16)
-            nc.scalar.copy(out=xs_of[g, i][:], in_=xb[:, g, D * i:D * (i + 1)].bitcast(FP8))
+            if g == 2:
+                nc.vector.tensor_copy(out=xs_of[g, i][:], in_=xb[:, g, D * i:D * (i + 1)].bitcast(FP8))
+            else:
+                nc.scalar.copy(out=xs_of[g, i][:], in_=xb[:, g, D * i:D * (i + 1)].bitcast(FP8))
 
         def prescale(g, i):
             if early(g, i):
@@ -195,8 +204,13 @@ def tile_gqaattention_pa_kernel(tc, x_bytes, x_scale, wq, wk, wv, gamma_q, gamma
                 nc.gpsimd.tensor_tensor(out=xw[:], in0=xs_of[g, i][:], in1=scale_bc[:], op=ALU.mult)
                 xs_of[g, i] = xw
 
-        def turn(g, i, tp=("tp", 2)):
-            xt_of[g, i] = turn_words(xs_of[g, i][:].bitcast(F32), tp)
+        def turn(g, i):
+            t = ring(banks, "tp", 1, [P, 2, 2, P], F32) if g >= 2 else ring(banks, "acc", 7, [P, 2, 2, P], F32)
+            words = xs_of[g, i][:].bitcast(F32)
+            for c in range(2):
+                for u in range(2):
+                    nc.tensor.transpose(t[:, u, c, :], words[:, 256 * c + u:256 * (c + 1):2], ident[:])
+            xt_of[g, i] = t
 
         def gather(g, i):
             if g not in xg_of:
@@ -205,14 +219,13 @@ def tile_gqaattention_pa_kernel(tc, x_bytes, x_scale, wq, wk, wv, gamma_q, gamma
             t = xt_of[g, i]
             if early(g, i):
                 nc.scalar.copy(out=xg[:, i].rearrange("p c r t -> p c (r t)").bitcast(F32).rearrange("p c (r u) -> p c r u", u=2),
-                               in_=t[:].rearrange("p c u r -> p c r u"))
+                               in_=t[:].rearrange("p u c r -> p c r u"))
             else:
-                for c in range(2):
-                    nc.vector.tensor_tensor(
-                        out=xg[:, i, c].rearrange("p r (u e) -> p r u e", u=2),
-                        in0=scale_t[:, c, :].rearrange("p (u e) -> p u e", u=2).unsqueeze(1).to_broadcast([P, P, 2, 2]),
-                        in1=t[:, c].rearrange("p u r -> p (u r)").bitcast(BF16).rearrange("p (u r e) -> p r u e", u=2, e=2),
-                        op=ALU.mult)
+                nc.vector.tensor_tensor(
+                    out=xg[:, i].rearrange("p c r (u e) -> p c r u e", u=2),
+                    in0=scale_t[:].rearrange("p c (u e) -> p c u e", u=2).unsqueeze(2).to_broadcast([P, 2, P, 2, 2]),
+                    in1=t[:].rearrange("p u c r -> p (u c r)").bitcast(BF16).rearrange("p (u c r e) -> p c r u e", u=2, c=2, e=2),
+                    op=ALU.mult)
 
         def quant(xg):
             xc = ring(rings, "xc", 4, [P, 512], U32, 64)
@@ -236,13 +249,13 @@ def tile_gqaattention_pa_kernel(tc, x_bytes, x_scale, wq, wk, wv, gamma_q, gamma
         ov_of = {}
 
         def where(j):
-            g, b = divmod(j, 3)
+            g, b = (j % 2, j // 2) if j < 6 else divmod(j, 3)
             return g, b, (4 if b < 2 else 2)
 
         def mx(j, i):
             g, b, nh = where(j)
             xc, xsc = xq[g]
-            acc = ring(banks, "acc", 6, [P, 512], F32)
+            acc = ring(banks, "acc", 7, [P, 512], F32)
             for c in range(2):
                 lc = slice(256 * i + P * c, 256 * i + P * (c + 1))
                 rc = slice(512 * b, 512 * (b + 1))
@@ -254,11 +267,28 @@ def tile_gqaattention_pa_kernel(tc, x_bytes, x_scale, wq, wk, wv, gamma_q, gamma
         def squares(j, i):
             g, b, nh = where(j)
             if i == 0:
-                ss_of[j] = ring(rings, "ss", 4, [P, 8], F32)
+                ss_of[j] = ss_early[:, 8 * j:8 * j + 8] if j < 2 else ring(rings, "ss", 4, [P, 8], F32)[:]
             for h in range(nh):
                 junk = ring(rings, "junk", 4, [P, HD], BF16)
                 nc.scalar.activation(out=junk[:], in_=acc_of[j, i][:, HD * h:HD * (h + 1)], func=ACT.Square,
                                      accum_out=ss_of[j][:, i * nh + h:i * nh + h + 1])
+
+        ss_early = keep.tile([P, 16], F32, name="ss_early")
+        nrm_early = keep.tile([P, 16], F32, name="nrm_early")
+        nrme_early = keep.tile([P, 16], F32, name="nrme_early")
+        rinv_early = keep.tile([P, 16], F32, name="rinv_early")
+
+        def early_norms():
+            nc.scalar.activation(out=nrm_early[:], in_=ss_early[:], func=ACT.Sqrt)
+            nc.scalar.activation(out=nrme_early[:], in_=nrm_early[:], func=ACT.Copy, bias=EPS)
+
+        def early_invert():
+            nc.vector.reciprocal(out=rinv_early[:], in_=nrme_early[:])
+
+        def scaling(n):
+            h, i, j = n % 4, n // 4 % 2, n // 8
+            nc.scalar.activation(out=o_of[j][:, h, i, :], in_=r_of[j][:, h, i, :], func=ACT.Copy,
+                                 scale=rinv_early[:, n // 4 * 4 + h:n // 4 * 4 + h + 1])
 
         def vcopy(j):
             g, b, nh = where(j)
@@ -284,12 +314,12 @@ def tile_gqaattention_pa_kernel(tc, x_bytes, x_scale, wq, wk, wv, gamma_q, gamma
             nc.vector.reciprocal(out=rinv_of[j][:, 0:n], in_=nrme_of[j][:, 0:n])
 
         def folded(j):
-            return j > 0
+            return j > 1
 
         def products(j, i):
             g, b, nh = where(j)
             if i == 0:
-                pr_of[j] = ring(rings, "pr", 3, [P, 4, 2, 4, HALF], F32)
+                pr_of[j] = ring(rings, "pr", 5, [P, 4, 2, 4, HALF], F32)
             pr = pr_of[j]
             if True:
                 gi = 2 * (g % 4) + i
@@ -308,24 +338,24 @@ def tile_gqaattention_pa_kernel(tc, x_bytes, x_scale, wq, wk, wv, gamma_q, gamma
                         in1=acc[:, 0:nh * HD].rearrange("p (h d) -> p h d", d=HD).unsqueeze(2).to_broadcast([P, nh, 2, HD]),
                         op=ALU.mult)
 
+        def adds_pair(j):
+            g, b, nh = where(j)
+            o_of[j] = ring(rings, "o", 5, [P, 4, 2, HD], F32)
+            pv = pr_of[j][:, 0:nh].rearrange("p h i (d s) j -> p (h i d) s j", s=2)
+            nc.gpsimd.tensor_tensor(out=o_of[j][:, 0:nh].rearrange("p h i (d j) -> p (h i d) j", d=2),
+                                    in0=pv[:, :, 0, :], in1=pv[:, :, 1, :], op=ALU.add)
+
         def adds(j, i):
             g, b, nh = where(j)
             if i == 0:
-                o_of[j] = ring(rings, "o", 5, [P, 4, 2, HD], F32)
+                o_of[j] = ring(rings, "o", 5, [P, 4, 2, HD], F32) if j > 1 else keep.tile([P, 4, 2, HD], F32, name="o_early%d" % j)
                 if not folded(j):
-                    r_of[j] = ring(rings, "r", 3, [P, 4, 2, HD], F32)
+                    r_of[j] = keep.tile([P, 4, 2, HD], F32, name="r_early%d" % j)
             r = o_of[j] if folded(j) else r_of[j]
             pv = pr_of[j][:, 0:nh, i].rearrange("p h (d s) j -> p h d s j", s=2)
-            eng = nc.vector if j == PAIRS - 1 else nc.gpsimd
+            eng = nc.vector if j == PAIRS - 1 or (j == PAIRS - 2 and i == 1) else nc.gpsimd
             eng.tensor_tensor(out=r[:, 0:nh, i, :].rearrange("p h (d j) -> p h d j", d=2),
                               in0=pv[:, :, :, 0, :], in1=pv[:, :, :, 1, :], op=ALU.add)
-
-        def scalings(j):
-            if not folded(j):
-                for h in range(4):
-                    for i in range(2):
-                        nc.scalar.activation(out=o_of[j][:, h, i, :], in_=r_of[j][:, h, i, :], func=ACT.Copy,
-                                             scale=rinv_of[j][:, i * 4 + h:i * 4 + h + 1])
 
         def vstore(j):
             g, b, nh = where(j)
@@ -344,14 +374,14 @@ def tile_gqaattention_pa_kernel(tc, x_bytes, x_scale, wq, wk, wv, gamma_q, gamma
                 nc.sync.dma_start(out=k_dst[bt][a], in_=ov[:, 0:2, :])
 
         def xwork(j, slot):
-            for g in range(2, GROUPS):
+            for g in range(3, GROUPS):
                 for what, when in XPLAN[early(g, 0)]:
                     if when == 4 * (j - 3 * g) + slot:
                         what(g)
 
         XPLAN = {
             True: ((lambda g: cast(g, 0), -34), (lambda g: prescale(g, 0), -31), (lambda g: cast(g, 1), -26), (lambda g: turn(g, 1), -21),
-                   (lambda g: gather(g, 1), -17), (lambda g: turn(g, 0), -17), (lambda g: gather(g, 0), -15), (lambda g: xquant(g), -13)),
+                   (lambda g: gather(g, 1), -17), (lambda g: turn(g, 0), -19), (lambda g: gather(g, 0), -17), (lambda g: xquant(g), -13)),
             False: ((lambda g: cast(g, 0), -30), (lambda g: cast(g, 1), -26), (lambda g: turn(g, 0), -25), (lambda g: gather(g, 0), -21), (lambda g: turn(g, 1), -21),
                     (lambda g: gather(g, 1), -17), (lambda g: xquant(g), -13)),
         }
@@ -359,125 +389,173 @@ def tile_gqaattention_pa_kernel(tc, x_bytes, x_scale, wq, wk, wv, gamma_q, gamma
         def xquant(g):
             xq[g] = quant(xg_of[g])
 
-        angles(0, 2)
+        angles(((0, 2), (2, 8)))
         cast(0, 0)
+        cast(0, 1)
         gam_copy()
         sines(0, 2)
-        cast(0, 1)
         gains(0, 2, 0)
-        gains(0, 2, 1)
-        angles(2, 8)
         wturn(0)
         wturn(1)
         turn(0, 0)
-        wturn(2)
         turn(0, 1)
+        wturn(2)
         wturn(3)
+        wturn(4)
+        wturn(5)
         wcopy(0, "V")
         wcopy(1, "S")
         gather(0, 0)
         wcopy(2, "S")
         gather(0, 1)
         wcopy(3, "S")
-        sines(2, 8)
-        gains(2, 8, 0)
+        cast(1, 0)
+        turn(1, 0)
+        cast(1, 1)
+        wcopy(4, "S")
         xq[0] = quant(xg_of[0])
         wquant(0)
-        for n in range(4, 8):
-            wturn(n)
         mx(0, 0)
         mx(0, 1)
-        wcopy(4, "S")
+        turn(1, 1)
+        wturn(6)
+        wturn(7)
+        sines(2, 8)
+        gains(2, 4, 0)
+        gains(4, 8, 0)
         wcopy(5, "S")
-        wcopy(6, "V")
-        wcopy(7, "S")
-        cast(1, 0)
-        wturn(8)
-        wturn(9)
-        turn(1, 0)
-        wquant(1)
-        squares(0, 0)
-        squares(0, 1)
-        mx(1, 0)
-        mx(1, 1)
+        gather(1, 0)
         products(0, 0)
         adds(0, 0)
         products(0, 1)
         adds(0, 1)
-        wcopy(8, "S")
-        wcopy(9, "S")
-        cast(1, 1)
-        gather(1, 0)
-        turn(1, 1)
+        squares(0, 0)
+        squares(0, 1)
+        gather(1, 1)
+        wcopy(6, "S")
+        wcopy(7, "S")
+        xq[1] = quant(xg_of[1])
+        cast(2, 0)
+        wquant(1)
+        cast(2, 1)
+        mx(1, 0)
+        mx(1, 1)
+        mx(2, 0)
+        mx(2, 1)
         squares(1, 0)
         squares(1, 1)
         nc.scalar.activation(out=first[:, 1:2], in_=sin2[:, 7, 1, 0:1], func=ACT.Sqrt, scale=0.0, bias=1.0)
-        root(1)
-        plus_eps(1)
-        wturn(10)
-        wturn(11)
-        gather(1, 1)
-        xq[1] = quant(xg_of[1])
-        invert(1)
         products(1, 0)
         adds(1, 0)
-        wcopy(10, "V")
-        wcopy(11, "S")
-        wquant(2)
         products(1, 1)
         adds(1, 1)
-        gains(2, 8, 1)
-        for s in range(-16, 4):
-            xwork(s // 4, s % 4)
-        mx(2, 0)
-        mx(2, 1)
+        gains(0, 2, 1)
+        gains(2, 4, 1)
+        gains(4, 8, 1)
         squares(2, 0)
         squares(2, 1)
         root(2)
-        vcopy(2)
+        turn(2, 0)
+        turn(2, 1)
         plus_eps(2)
-        root(0)
-        plus_eps(0)
-        vstore(2)
-        for s in range(4, 8):
-            xwork(s // 4, s % 4)
+        wturn(8)
+        wturn(9)
+        gather(2, 0)
+        gather(2, 1)
         invert(2)
-        invert(0)
-        scalings(0)
-        store(0)
-        store(1)
         mx(3, 0)
         mx(3, 1)
+        wcopy(8, "S")
+        wcopy(9, "S")
+        products(2, 0)
+        adds(2, 0)
+        products(2, 1)
+        adds(2, 1)
+        wturn(10, ("tp", 1))
+        wturn(11)
+        wcopy(10, "S")
+        wcopy(11, "S")
         squares(3, 0)
         squares(3, 1)
         root(3)
-        plus_eps(3)
+        wquant(2)
+        xq[2] = quant(xg_of[2])
         mx(4, 0)
+        mx(4, 1)
+        mx(5, 0)
+        mx(5, 1)
+        plus_eps(3)
+        invert(3)
+        for s in range(-8, 8):
+            xwork(s // 4, s % 4)
+        products(3, 0)
+        adds(3, 0)
+        products(3, 1)
+        adds(3, 1)
+        squares(4, 0)
+        squares(4, 1)
+        root(4)
+        vcopy(4)
+        plus_eps(4)
+        vstore(4)
+        for s in range(8, 12):
+            xwork(s // 4, s % 4)
+        mx(6, 0)
+        mx(6, 1)
+        mx(7, 0)
+        invert(4)
+        squares(5, 0)
+        squares(5, 1)
+        root(5)
+        vcopy(5)
+        plus_eps(5)
+        vstore(5)
+        squares(6, 0)
+        store(2)
+        store(3)
 
-        for j in range(2, PAIRS + 1):
-            if j + 2 < PAIRS:
-                mx(j + 2, 1)
-                squares(j + 2, 0)
-            xwork(j, 0)
-            if j < PAIRS:
-                products(j, 0)
-                adds(j, 0)
-            xwork(j, 1)
-            if j + 3 < PAIRS:
+        for j in range(4, PAIRS + 1):
+            if j + 3 < PAIRS and j > 4:
                 mx(j + 3, 0)
             if j + 2 < PAIRS:
                 squares(j + 2, 1)
+            xwork(j, 0)
+            if j < PAIRS:
+                products(j, 0)
+                if not (lambda n: n % 3 == 2 and n < 23)(j):
+                    adds(j, 0)
+            if j == 4:
+                for s in range(12, 16):
+                    xwork(s // 4, s % 4)
+            xwork(j, 1)
+            if j + 3 < PAIRS:
+                mx(j + 3, 1)
+                squares(j + 3, 0)
+            if j + 2 < PAIRS:
                 root(j + 2)
                 vcopy(j + 2)
-            xwork(j, 2)
+            pass
             if j + 2 < PAIRS:
                 plus_eps(j + 2)
                 vstore(j + 2)
+            xwork(j, 2)
+            if j == 20:
+                early_norms()
+            if j == 21:
+                early_invert()
+            if j == 22:
+                for n in range(16):
+                    scaling(n)
+                store(0)
+                store(1)
             if j + 1 < PAIRS:
                 invert(j + 1)
             if j < PAIRS:
                 products(j, 1)
-                adds(j, 1)
+                if (lambda n: n % 3 == 2 and n < 23)(j):
+                    adds_pair(j)
+                else:
+                    adds(j, 1)
             xwork(j, 3)
-            if j > 2:
+            if j > 4:
                 store(j - 1)

@@ -58,7 +58,6 @@ def tile_gqaattention_pa_kernel(tc, x_bytes, x_scale, wq, wk, wv, gamma_q, gamma
         xb = keep.tile([P, GROUPS, 2 * D], U8, name="x_bytes_sb")
         x_rows = x_bytes.rearrange("b t k -> (b t) k").rearrange("(g p i) k -> p g (i k)", p=P, i=2)
         scale_t = keep.tile([P, 2, 4], F32, name="scale_t")
-        scale_bc = keep.tile([P, D], F32, name="scale_bc")
         wraw = keep.tile([P, 12, D], BF16, name="wraw")
         gam_rows = keep.tile([P, 2 * HD], BF16, name="gam_rows")
         nc.vector.memset(gam_rows[:], 0.0)
@@ -83,7 +82,6 @@ def tile_gqaattention_pa_kernel(tc, x_bytes, x_scale, wq, wk, wv, gamma_q, gamma
         nc.sync.dma_start(out=xb[:, 2:4, :], in_=x_rows[:, 2:4, :])
         nc.sync.dma_start(out=xb[:, 4:8, :], in_=x_rows[:, 4:8, :])
 
-        nc.sync.dma_start(out=scale_bc[:], in_=x_scale.rearrange("a b k -> (a b k)").partition_broadcast(P))
 
         tpos = keep.tile([P, 8], F32, name="tpos")
         nc.gpsimd.iota(tpos[:], pattern=[[256, 4], [1, 2]], base=0, channel_multiplier=2,
@@ -184,9 +182,6 @@ def tile_gqaattention_pa_kernel(tc, x_bytes, x_scale, wq, wk, wv, gamma_q, gamma
                 nc.vector.quantize_mx(out=wc[:, c, cols].bitcast(FP8X4), scales=wsc[:, c, cols],
                                       in_=wg[:, c].rearrange("p f u -> p (f u)").bitcast(BF16))
 
-        def early(g, i):
-            return False
-
         xs_of = {}
         xt_of = {}
         xg_of = {}
@@ -197,12 +192,6 @@ def tile_gqaattention_pa_kernel(tc, x_bytes, x_scale, wq, wk, wv, gamma_q, gamma
                 nc.vector.tensor_copy(out=xs_of[g, i][:], in_=xb[:, g, D * i:D * (i + 1)].bitcast(FP8))
             else:
                 nc.scalar.copy(out=xs_of[g, i][:], in_=xb[:, g, D * i:D * (i + 1)].bitcast(FP8))
-
-        def prescale(g, i):
-            if early(g, i):
-                xw = ring(rings, "xw", 2, [P, D], BF16)
-                nc.gpsimd.tensor_tensor(out=xw[:], in0=xs_of[g, i][:], in1=scale_bc[:], op=ALU.mult)
-                xs_of[g, i] = xw
 
         def turn(g, i):
             t = ring(banks, "tp", 1, [P, 2, 2, P], F32) if g >= 2 else ring(banks, "acc", 7, [P, 2, 2, P], F32)
@@ -217,15 +206,11 @@ def tile_gqaattention_pa_kernel(tc, x_bytes, x_scale, wq, wk, wv, gamma_q, gamma
                 xg_of[g] = ring(rings, "xg", 2, [P, 2, 2, P, 4], BF16, 64)
             xg = xg_of[g]
             t = xt_of[g, i]
-            if early(g, i):
-                nc.scalar.copy(out=xg[:, i].rearrange("p c r t -> p c (r t)").bitcast(F32).rearrange("p c (r u) -> p c r u", u=2),
-                               in_=t[:].rearrange("p u c r -> p c r u"))
-            else:
-                nc.vector.tensor_tensor(
-                    out=xg[:, i].rearrange("p c r (u e) -> p c r u e", u=2),
-                    in0=scale_t[:].rearrange("p c (u e) -> p c u e", u=2).unsqueeze(2).to_broadcast([P, 2, P, 2, 2]),
-                    in1=t[:].rearrange("p u c r -> p (u c r)").bitcast(BF16).rearrange("p (u c r e) -> p c r u e", u=2, c=2, e=2),
-                    op=ALU.mult)
+            nc.vector.tensor_tensor(
+                out=xg[:, i].rearrange("p c r (u e) -> p c r u e", u=2),
+                in0=scale_t[:].rearrange("p c (u e) -> p c u e", u=2).unsqueeze(2).to_broadcast([P, 2, P, 2, 2]),
+                in1=t[:].rearrange("p u c r -> p (u c r)").bitcast(BF16).rearrange("p (u c r e) -> p c r u e", u=2, c=2, e=2),
+                op=ALU.mult)
 
         def quant(xg):
             xc = ring(rings, "xc", 4, [P, 512], U32, 64)
@@ -375,19 +360,15 @@ def tile_gqaattention_pa_kernel(tc, x_bytes, x_scale, wq, wk, wv, gamma_q, gamma
 
         def xwork(j, slot):
             for g in range(3, GROUPS):
-                for what, when in XPLAN[early(g, 0)]:
+                for what, when in XPLAN:
                     if when == 4 * (j - 3 * g) + slot:
                         what(g)
 
-        XPLAN = {
-            True: ((lambda g: cast(g, 0), -34), (lambda g: prescale(g, 0), -31), (lambda g: cast(g, 1), -26), (lambda g: turn(g, 1), -21),
-                   (lambda g: gather(g, 1), -17), (lambda g: turn(g, 0), -19), (lambda g: gather(g, 0), -17), (lambda g: xquant(g), -13)),
-            False: ((lambda g: cast(g, 0), -30), (lambda g: cast(g, 1), -26), (lambda g: turn(g, 0), -25), (lambda g: gather(g, 0), -21), (lambda g: turn(g, 1), -21),
-                    (lambda g: gather(g, 1), -17), (lambda g: xquant(g), -13)),
-        }
-
         def xquant(g):
             xq[g] = quant(xg_of[g])
+
+        XPLAN = ((lambda g: cast(g, 0), -30), (lambda g: cast(g, 1), -26), (lambda g: turn(g, 0), -25), (lambda g: gather(g, 0), -21),
+                 (lambda g: turn(g, 1), -21), (lambda g: gather(g, 1), -17), (lambda g: xquant(g), -13))
 
         angles(((0, 2), (2, 8)))
         cast(0, 0)

@@ -58,6 +58,7 @@ def tile_gqaattention_pa_kernel(tc, x_bytes, x_scale, wq, wk, wv, gamma_q, gamma
         xb = keep.tile([P, GROUPS, 2 * D], U8, name="x_bytes_sb")
         x_rows = x_bytes.rearrange("b t k -> (b t) k").rearrange("(g p i) k -> p g (i k)", p=P, i=2)
         scale_t = keep.tile([P, 2, 4], F32, name="scale_t")
+        scale_bc = keep.tile([P, D], F32, name="scale_bc")
         wraw = keep.tile([P, 12, D], BF16, name="wraw")
         gam_rows = keep.tile([P, 2 * HD], BF16, name="gam_rows")
         nc.vector.memset(gam_rows[:], 0.0)
@@ -82,6 +83,8 @@ def tile_gqaattention_pa_kernel(tc, x_bytes, x_scale, wq, wk, wv, gamma_q, gamma
         nc.sync.dma_start(out=xb[:, 2:4, :], in_=x_rows[:, 2:4, :])
         nc.sync.dma_start(out=xb[:, 4:8, :], in_=x_rows[:, 4:8, :])
 
+
+        nc.sync.dma_start(out=scale_bc[:], in_=x_scale.rearrange("a b k -> (a b k)").partition_broadcast(P))
 
         tpos = keep.tile([P, 8], F32, name="tpos")
         nc.gpsimd.iota(tpos[:], pattern=[[256, 4], [1, 2]], base=0, channel_multiplier=2,
@@ -193,8 +196,16 @@ def tile_gqaattention_pa_kernel(tc, x_bytes, x_scale, wq, wk, wv, gamma_q, gamma
             else:
                 nc.scalar.copy(out=xs_of[g, i][:], in_=xb[:, g, D * i:D * (i + 1)].bitcast(FP8))
 
+        def early(g, i):
+            return i == 0 and g in (5, 7)
+
+        def prescale(g, i):
+            xw = ring(rings, "xw", 2, [P, D], BF16)
+            nc.gpsimd.tensor_tensor(out=xw[:], in0=xs_of[g, i][:], in1=scale_bc[:], op=ALU.mult)
+            xs_of[g, i] = xw
+
         def turn(g, i):
-            t = ring(banks, "tp", 1, [P, 2, 2, P], F32) if g >= 2 else ring(banks, "acc", 7, [P, 2, 2, P], F32)
+            t = ring(banks, "tp", 1, [P, 2, 2, P], F32) if g >= 3 or (g == 2 and i == 0) else ring(banks, "acc", 7, [P, 2, 2, P], F32)
             words = xs_of[g, i][:].bitcast(F32)
             for c in range(2):
                 for u in range(2):
@@ -206,6 +217,10 @@ def tile_gqaattention_pa_kernel(tc, x_bytes, x_scale, wq, wk, wv, gamma_q, gamma
                 xg_of[g] = ring(rings, "xg", 2, [P, 2, 2, P, 4], BF16, 64)
             xg = xg_of[g]
             t = xt_of[g, i]
+            if early(g, i):
+                nc.scalar.copy(out=xg[:, i].rearrange("p c r t -> p c (r t)").bitcast(F32).rearrange("p c (r u) -> p c r u", u=2),
+                               in_=t[:].rearrange("p u c r -> p c r u"))
+                return
             nc.vector.tensor_tensor(
                 out=xg[:, i].rearrange("p c r (u e) -> p c r u e", u=2),
                 in0=scale_t[:].rearrange("p c (u e) -> p c u e", u=2).unsqueeze(2).to_broadcast([P, 2, P, 2, 2]),
@@ -360,23 +375,28 @@ def tile_gqaattention_pa_kernel(tc, x_bytes, x_scale, wq, wk, wv, gamma_q, gamma
 
         def xwork(j, slot):
             for g in range(3, GROUPS):
-                for what, when in XPLAN:
+                for what, when in XPLAN[early(g, 0)]:
                     if when == 4 * (j - 3 * g) + slot:
                         what(g)
 
         def xquant(g):
             xq[g] = quant(xg_of[g])
 
-        XPLAN = ((lambda g: cast(g, 0), -30), (lambda g: cast(g, 1), -26), (lambda g: turn(g, 0), -25), (lambda g: gather(g, 0), -21),
-                 (lambda g: turn(g, 1), -21), (lambda g: gather(g, 1), -17), (lambda g: xquant(g), -13))
+        XPLAN = {
+            True: ((lambda g: cast(g, 0), -34), (lambda g: prescale(g, 0), -31), (lambda g: cast(g, 1), -26), (lambda g: turn(g, 0), -25),
+                   (lambda g: gather(g, 0), -23), (lambda g: turn(g, 1), -21), (lambda g: gather(g, 1), -17), (lambda g: xquant(g), -13)),
+            False: ((lambda g: cast(g, 0), -30), (lambda g: cast(g, 1), -26), (lambda g: turn(g, 0), -25), (lambda g: gather(g, 0), -21),
+                    (lambda g: turn(g, 1), -21), (lambda g: gather(g, 1), -17), (lambda g: xquant(g), -13)),
+        }
 
         angles(((0, 2), (2, 8)))
         cast(0, 0)
         cast(0, 1)
         gam_copy()
+        wturn(0)
+        wcopy(0, "S")
         sines(0, 2)
         gains(0, 2, 0)
-        wturn(0)
         wturn(1)
         turn(0, 0)
         turn(0, 1)
@@ -384,7 +404,6 @@ def tile_gqaattention_pa_kernel(tc, x_bytes, x_scale, wq, wk, wv, gamma_q, gamma
         wturn(3)
         wturn(4)
         wturn(5)
-        wcopy(0, "V")
         wcopy(1, "S")
         gather(0, 0)
         wcopy(2, "S")
@@ -401,6 +420,8 @@ def tile_gqaattention_pa_kernel(tc, x_bytes, x_scale, wq, wk, wv, gamma_q, gamma
         turn(1, 1)
         wturn(6)
         wturn(7)
+        for n in range(8, 12):
+            wturn(n)
         sines(2, 8)
         gains(2, 4, 0)
         gains(4, 8, 0)
@@ -415,6 +436,8 @@ def tile_gqaattention_pa_kernel(tc, x_bytes, x_scale, wq, wk, wv, gamma_q, gamma
         gather(1, 1)
         wcopy(6, "S")
         wcopy(7, "S")
+        wcopy(8, "S")
+        wcopy(9, "S")
         xq[1] = quant(xg_of[1])
         cast(2, 0)
         wquant(1)
@@ -439,23 +462,17 @@ def tile_gqaattention_pa_kernel(tc, x_bytes, x_scale, wq, wk, wv, gamma_q, gamma
         turn(2, 0)
         turn(2, 1)
         plus_eps(2)
-        wturn(8)
-        wturn(9)
+        wcopy(10, "S")
+        wcopy(11, "S")
         gather(2, 0)
         gather(2, 1)
         invert(2)
         mx(3, 0)
         mx(3, 1)
-        wcopy(8, "S")
-        wcopy(9, "S")
         products(2, 0)
         adds(2, 0)
         products(2, 1)
         adds(2, 1)
-        wturn(10, ("tp", 1))
-        wturn(11)
-        wcopy(10, "S")
-        wcopy(11, "S")
         squares(3, 0)
         squares(3, 1)
         root(3)

@@ -58,7 +58,6 @@ def tile_gqaattention_pa_kernel(tc, x_bytes, x_scale, wq, wk, wv, gamma_q, gamma
         xb = keep.tile([P, GROUPS, 2 * D], U8, name="x_bytes_sb")
         x_rows = x_bytes.rearrange("b t k -> (b t) k").rearrange("(g p i) k -> p g (i k)", p=P, i=2)
         scale_t = keep.tile([P, 2, 4], F32, name="scale_t")
-        scale_bc = keep.tile([P, D], F32, name="scale_bc")
         wraw = keep.tile([P, 12, D], BF16, name="wraw")
         gam_rows = keep.tile([P, 2 * HD], BF16, name="gam_rows")
         nc.vector.memset(gam_rows[:], 0.0)
@@ -83,8 +82,6 @@ def tile_gqaattention_pa_kernel(tc, x_bytes, x_scale, wq, wk, wv, gamma_q, gamma
         nc.sync.dma_start(out=xb[:, 2:4, :], in_=x_rows[:, 2:4, :])
         nc.sync.dma_start(out=xb[:, 4:8, :], in_=x_rows[:, 4:8, :])
 
-
-        nc.sync.dma_start(out=scale_bc[:], in_=x_scale.rearrange("a b k -> (a b k)").partition_broadcast(P))
 
         tpos = keep.tile([P, 8], F32, name="tpos")
         nc.gpsimd.iota(tpos[:], pattern=[[256, 4], [1, 2]], base=0, channel_multiplier=2,
@@ -196,14 +193,6 @@ def tile_gqaattention_pa_kernel(tc, x_bytes, x_scale, wq, wk, wv, gamma_q, gamma
             else:
                 nc.scalar.copy(out=xs_of[g, i][:], in_=xb[:, g, D * i:D * (i + 1)].bitcast(FP8))
 
-        def early(g, i):
-            return i == 0 and g in (5, 7)
-
-        def prescale(g, i):
-            xw = ring(rings, "xw", 2, [P, D], BF16)
-            nc.gpsimd.tensor_tensor(out=xw[:], in0=xs_of[g, i][:], in1=scale_bc[:], op=ALU.mult)
-            xs_of[g, i] = xw
-
         def turn(g, i):
             t = ring(banks, "tp", 1, [P, 2, 2, P], F32) if g >= 3 or (g == 2 and i == 0) else ring(banks, "acc", 7, [P, 2, 2, P], F32)
             words = xs_of[g, i][:].bitcast(F32)
@@ -217,10 +206,6 @@ def tile_gqaattention_pa_kernel(tc, x_bytes, x_scale, wq, wk, wv, gamma_q, gamma
                 xg_of[g] = ring(rings, "xg", 2, [P, 2, 2, P, 4], BF16, 64)
             xg = xg_of[g]
             t = xt_of[g, i]
-            if early(g, i):
-                nc.scalar.copy(out=xg[:, i].rearrange("p c r t -> p c (r t)").bitcast(F32).rearrange("p c (r u) -> p c r u", u=2),
-                               in_=t[:].rearrange("p u c r -> p c r u"))
-                return
             nc.vector.tensor_tensor(
                 out=xg[:, i].rearrange("p c r (u e) -> p c r u e", u=2),
                 in0=scale_t[:].rearrange("p c (u e) -> p c u e", u=2).unsqueeze(2).to_broadcast([P, 2, P, 2, 2]),
@@ -375,19 +360,15 @@ def tile_gqaattention_pa_kernel(tc, x_bytes, x_scale, wq, wk, wv, gamma_q, gamma
 
         def xwork(j, slot):
             for g in range(3, GROUPS):
-                for what, when in XPLAN[early(g, 0)]:
+                for what, when in XPLAN:
                     if when == 4 * (j - 3 * g) + slot:
                         what(g)
 
         def xquant(g):
             xq[g] = quant(xg_of[g])
 
-        XPLAN = {
-            True: ((lambda g: cast(g, 0), -34), (lambda g: prescale(g, 0), -31), (lambda g: cast(g, 1), -26), (lambda g: turn(g, 0), -25),
-                   (lambda g: gather(g, 0), -23), (lambda g: turn(g, 1), -21), (lambda g: gather(g, 1), -17), (lambda g: xquant(g), -13)),
-            False: ((lambda g: cast(g, 0), -30), (lambda g: cast(g, 1), -26), (lambda g: turn(g, 0), -25), (lambda g: gather(g, 0), -21),
-                    (lambda g: turn(g, 1), -21), (lambda g: gather(g, 1), -17), (lambda g: xquant(g), -13)),
-        }
+        XPLAN = ((lambda g: cast(g, 0), -30), (lambda g: cast(g, 1), -26), (lambda g: turn(g, 0), -25), (lambda g: gather(g, 0), -21),
+                 (lambda g: turn(g, 1), -21), (lambda g: gather(g, 1), -17), (lambda g: xquant(g), -13))
 
         angles(((0, 2), (2, 8)))
         cast(0, 0)

@@ -275,6 +275,12 @@ def tile_gqaattention_pa_kernel(tc, x_bytes, x_scale, wq, wk, wv, gamma_q, gamma
             nc.scalar.activation(out=o_of[j][:, h, i, :], in_=r_of[j][:, h, i, :], func=ACT.Copy,
                                  scale=rinv_early[:, n // 4 * 4 + h:n // 4 * 4 + h + 1])
 
+        def rescale(j):
+            for i in range(2):
+                for h in range(4):
+                    nc.scalar.activation(out=o_of[j][:, h, i, :], in_=r_of[j][:, h, i, :], func=ACT.Copy,
+                                         scale=rinv_of[j][:, i * 4 + h:i * 4 + h + 1])
+
         def vcopy(j):
             g, b, nh = where(j)
             if b == 2:
@@ -295,11 +301,14 @@ def tile_gqaattention_pa_kernel(tc, x_bytes, x_scale, wq, wk, wv, gamma_q, gamma
 
         def invert(j):
             n = 2 * where(j)[2]
-            rinv_of[j] = ring(rings, "rinv", 4, [P, 8], F32)
+            rinv_of[j] = ring(rings, "rinv", 7, [P, 8], F32)
             nc.vector.reciprocal(out=rinv_of[j][:, 0:n], in_=nrme_of[j][:, 0:n])
 
+        def UNF(j):
+            return j < 2
+
         def folded(j):
-            return j > 1
+            return not UNF(j)
 
         def products(j, i):
             g, b, nh = where(j)
@@ -325,7 +334,7 @@ def tile_gqaattention_pa_kernel(tc, x_bytes, x_scale, wq, wk, wv, gamma_q, gamma
 
         def adds_pair(j):
             g, b, nh = where(j)
-            o_of[j] = ring(rings, "o", 5, [P, 4, 2, HD], F32)
+            o_of[j] = ring(rings, "o", 6, [P, 4, 2, HD], F32)
             pv = pr_of[j][:, 0:nh].rearrange("p h i (d s) j -> p (h i d) s j", s=2)
             nc.gpsimd.tensor_tensor(out=o_of[j][:, 0:nh].rearrange("p h i (d j) -> p (h i d) j", d=2),
                                     in0=pv[:, :, 0, :], in1=pv[:, :, 1, :], op=ALU.add)
@@ -333,9 +342,9 @@ def tile_gqaattention_pa_kernel(tc, x_bytes, x_scale, wq, wk, wv, gamma_q, gamma
         def adds(j, i):
             g, b, nh = where(j)
             if i == 0:
-                o_of[j] = ring(rings, "o", 5, [P, 4, 2, HD], F32) if j > 1 else keep.tile([P, 4, 2, HD], F32, name="o_early%d" % j)
+                o_of[j] = ring(rings, "o", 6, [P, 4, 2, HD], F32) if j > 1 else keep.tile([P, 4, 2, HD], F32, name="o_early%d" % j)
                 if not folded(j):
-                    r_of[j] = keep.tile([P, 4, 2, HD], F32, name="r_early%d" % j)
+                    r_of[j] = ring(rings, "r", 3, [P, 4, 2, HD], F32) if j > 1 else keep.tile([P, 4, 2, HD], F32, name="r_early%d" % j)
             r = o_of[j] if folded(j) else r_of[j]
             pv = pr_of[j][:, 0:nh, i].rearrange("p h (d s) j -> p h d s j", s=2)
             eng = nc.vector if j == PAIRS - 1 or (j == PAIRS - 2 and i == 1) else nc.gpsimd
@@ -518,15 +527,18 @@ def tile_gqaattention_pa_kernel(tc, x_bytes, x_scale, wq, wk, wv, gamma_q, gamma
                 plus_eps(j + 2)
                 vstore(j + 2)
             xwork(j, 2)
-            if j == 20:
+            if j - 2 > 1 and j - 2 < PAIRS and not folded(j - 2):
+                rescale(j - 2)
+                store(j - 2)
+            if j == 5:
                 early_norms()
-            if j == 21:
+            if j == 7:
                 early_invert()
-            if j == 22:
-                for n in range(16):
-                    scaling(n)
-                store(0)
-                store(1)
+            if j in (9, 15):
+                u = (j - 9) // 6
+                for n in range(8):
+                    scaling(8 * u + n)
+                store(u)
             if j + 1 < PAIRS:
                 invert(j + 1)
             if j < PAIRS:
@@ -536,5 +548,5 @@ def tile_gqaattention_pa_kernel(tc, x_bytes, x_scale, wq, wk, wv, gamma_q, gamma
                 else:
                     adds(j, 1)
             xwork(j, 3)
-            if j > 4:
+            if j > 4 and folded(j - 1):
                 store(j - 1)

from contextlib import ExitStack

import concourse.mybir as mybir
from concourse.masks import make_identity

F32 = mybir.dt.float32
BF16 = mybir.dt.bfloat16
U32 = mybir.dt.uint32
U8 = mybir.dt.uint8
I32 = mybir.dt.int32
FP8 = mybir.dt.float8_e4m3fn
FP8X4 = mybir.dt.float8_e4m3fn_x4
ALU = mybir.AluOpType
ACT = mybir.ActivationFunctionType

P = 128
D = 1024
HD = 128
HALF = 64
ROPE_BASE = 10000.0
EPS = 1e-6
GROUPS = 8
PAIRS = 24
TWO_PI = 6.283185307179586
LEAD = 2
XCAST = 5
XPROD = 4
XQ = 3
XG = 6
SPLIT = 2
XO = -3

FLOPS = 2 * 2048 * 1024 * 1536


def tile_gqaattention_pa_kernel(tc, x_bytes, x_scale, wq, wk, wv, gamma_q, gamma_k, out_0, out_1, out_2):
    nc = tc.nc
    with ExitStack() as ctx:
        keep = ctx.enter_context(tc.tile_pool(name="keep", bufs=1))
        rings = ctx.enter_context(tc.tile_pool(name="rings", bufs=1))
        banks = ctx.enter_context(tc.psum_pool(name="banks", bufs=1))
        ctx.enter_context(tc.manual_schedule())
        taken = {}

        def ring(pool, base, depth, shape, dtype, align=None):
            k = taken.get(base, 0)
            taken[base] = k + 1
            slot = "%s%d" % (base, k % depth)
            if align is None:
                return pool.tile(shape, dtype, name=slot)
            return pool.tile(shape, dtype, name=slot, align_bytes=align)

        one = keep.tile([P, 1], F32, name="one")
        nc.vector.memset(one[:], 1.0)
        first = keep.tile([P, 2], F32, name="first")
        nc.scalar.activation(out=first[:, 0:1], in_=one[:], func=ACT.Sin)

        xb = keep.tile([P, GROUPS, 2 * D], U8, name="x_bytes_sb")
        x_rows = x_bytes.rearrange("b t k -> (b t) k").rearrange("(g p i) k -> p g (i k)", p=P, i=2)
        scale_t = keep.tile([P, 2, 4], F32, name="scale_t")
        wraw = keep.tile([P, 12, D], BF16, name="wraw")
        gam_rows = keep.tile([P, 2 * HD], BF16, name="gam_rows")
        nc.vector.memset(gam_rows[:], 0.0)
        ones_sq = keep.tile([P, P], BF16, name="ones_sq")
        nc.vector.memset(ones_sq[:], 1.0)
        gam = keep.tile([P, 2, HD], F32, name="gam")
        wq_rows = wq.rearrange("(a p) k -> p a k", p=P)

        nc.sync.dma_start(out=xb[:, 0:1, :], in_=x_rows[:, 0:1, :])
        nc.sync.dma_start(out=gam_rows[0:1, 0:HD], in_=gamma_q.unsqueeze(0))
        nc.sync.dma_start(out=gam_rows[0:1, HD:2 * HD], in_=gamma_k.unsqueeze(0))
        with nc.allow_non_contiguous_dma(reason="four scales to a partition and pass"):
            nc.sync.dma_start(out=scale_t[:], in_=x_scale.rearrange("a b (c p t) -> p (a b c) t", p=P, t=4))
        nc.sync.dma_start(out=wraw[:, 0:1, :], in_=wq_rows[:, 0:1, :])
        nc.sync.dma_start(out=wraw[:, 1:2, :], in_=wq_rows[:, 1:2, :])
        nc.sync.dma_start(out=wraw[:, 2:4, :], in_=wq_rows[:, 2:4, :])
        nc.sync.dma_start(out=xb[:, 1:2, :], in_=x_rows[:, 1:2, :])
        nc.sync.dma_start(out=wraw[:, 4:6, :], in_=wq_rows[:, 4:6, :])
        nc.sync.dma_start(out=wraw[:, 6:8, :], in_=wq_rows[:, 6:8, :])
        nc.sync.dma_start(out=wraw[:, 8:10, :], in_=wk.rearrange("(a p) k -> p a k", p=P))
        nc.sync.dma_start(out=wraw[:, 10:12, :], in_=wv.rearrange("(a p) k -> p a k", p=P))
        nc.sync.dma_start(out=xb[:, 2:4, :], in_=x_rows[:, 2:4, :])
        nc.sync.dma_start(out=xb[:, 4:8, :], in_=x_rows[:, 4:8, :])


        tpos = keep.tile([P, 8], F32, name="tpos")
        nc.gpsimd.iota(tpos[:], pattern=[[256, 4], [1, 2]], base=0, channel_multiplier=2,
                       allow_small_or_imprecise_dtypes=True)
        ident = keep.tile([P, P], F32, name="ident")
        make_identity(nc, ident[:])

        gam_ps = ring(banks, "tp", 1, [P, 2, 2, P], F32)
        nc.tensor.matmul(out=gam_ps[:, 0].rearrange("p u r -> p (u r)"), lhsT=ones_sq[:], rhs=gam_rows[:], start=True, stop=True)

        def gam_copy():
            nc.scalar.copy(out=gam[:].rearrange("p w d -> p (w d)"), in_=gam_ps[:, 0].rearrange("p u r -> p (u r)"))


        turns = keep.tile([P, 8], F32, name="turns")
        nc.vector.tensor_scalar(out=turns[:], in0=tpos[:], scalar1=1.0 / TWO_PI, scalar2=None, op0=ALU.mult)
        freq = keep.tile([P, HALF], F32, name="freq")
        nc.vector.memset(freq[:, 0:1], 1.0)
        for m in (1, 2, 4, 8, 16, 32):
            nc.vector.tensor_scalar(out=freq[:, m:2 * m], in0=freq[:, 0:m], scalar1=ROPE_BASE ** (-m / HALF),
                                    scalar2=None, op0=ALU.mult)
        phi = keep.tile([P, 8, HALF], F32, name="phi")
        whole_i = keep.tile([P, 8 * HALF], I32, name="whole_i")
        whole = keep.tile([P, 8 * HALF], F32, name="whole")
        frac = keep.tile([P, 8 * HALF], F32, name="frac")
        negs = keep.tile([P, 8, HALF], F32, name="negs")
        cq = keep.tile([P, 8 * HALF], F32, name="cq")
        negc = keep.tile([P, 8, HALF], F32, name="negc")
        cos_t = keep.tile([P, 8, HALF], F32, name="cos_t")
        sin2 = keep.tile([P, 8, 2, HALF], F32, name="sin2")

        def angles(spans):
            def each(f):
                for lo, hi in spans:
                    f(lo, hi, slice(HALF * lo, HALF * hi))

            phi_f = phi[:].rearrange("p a j -> p (a j)")
            negs_f = negs[:].rearrange("p a j -> p (a j)")
            negc_f = negc[:].rearrange("p a j -> p (a j)")
            each(lambda lo, hi, c: nc.vector.tensor_tensor(
                out=phi[:, lo:hi, :], in0=turns[:, lo:hi].unsqueeze(2).to_broadcast([P, hi - lo, HALF]),
                in1=freq[:].unsqueeze(1).to_broadcast([P, hi - lo, HALF]), op=ALU.mult))
            each(lambda lo, hi, c: nc.vector.tensor_copy(out=whole_i[:, c], in_=phi_f[:, c]))
            each(lambda lo, hi, c: nc.vector.tensor_copy(out=whole[:, c], in_=whole_i[:, c]))
            each(lambda lo, hi, c: nc.vector.tensor_tensor(out=frac[:, c], in0=phi_f[:, c], in1=whole[:, c], op=ALU.subtract))
            each(lambda lo, hi, c: nc.vector.scalar_tensor_tensor(out=negs_f[:, c], in0=frac[:, c], scalar=0.5, in1=frac[:, c],
                                                                  op0=ALU.is_gt, op1=ALU.subtract))
            each(lambda lo, hi, c: nc.vector.tensor_scalar(out=cq[:, c], in0=negs_f[:, c], scalar1=-1.0, scalar2=0.25,
                                                           op0=ALU.mult, op1=ALU.add))
            each(lambda lo, hi, c: nc.vector.scalar_tensor_tensor(out=negc_f[:, c], in0=cq[:, c], scalar=0.5, in1=cq[:, c],
                                                                  op0=ALU.is_gt, op1=ALU.subtract))

        def sines(lo, hi):
            nc.scalar.activation(out=cos_t[:, lo:hi, :], in_=negc[:, lo:hi, :], func=ACT.Sin, scale=-TWO_PI)
            nc.scalar.activation(out=sin2[:, lo:hi, 0, :], in_=negs[:, lo:hi, :], func=ACT.Sin, scale=TWO_PI)
            nc.scalar.activation(out=sin2[:, lo:hi, 1, :], in_=negs[:, lo:hi, :], func=ACT.Sin, scale=-TWO_PI)

        rope = keep.tile([P, 2, 8, 4, HALF], F32, name="rope")

        def gains(lo, hi, w):
            n = hi - lo
            gv = gam[:, w, :].rearrange("p (s j) -> p s j", s=2).unsqueeze(1).to_broadcast([P, n, 2, HALF])
            nc.gpsimd.tensor_tensor(out=rope[:, w, lo:hi, 0:4:3, :],
                                    in0=cos_t[:, lo:hi, :].unsqueeze(2).to_broadcast([P, n, 2, HALF]), in1=gv, op=ALU.mult)
            nc.gpsimd.tensor_tensor(out=rope[:, w, lo:hi, 1:3, :], in0=sin2[:, lo:hi, :, :], in1=gv, op=ALU.mult)

        wc = keep.tile([P, 2, 1536], U32, name="wc", align_bytes=64)
        wsc = keep.tile([P, 2, 1536], U8, name="wsc", align_bytes=64)

        def turn_words(words, tp):
            t = ring(banks, tp[0], tp[1], [P, 2, 2, P], F32)
            for c in range(2):
                for u in range(2):
                    nc.tensor.transpose(t[:, c, u, :], words[:, 256 * c + u:256 * (c + 1):2], ident[:])
            return t

        wg_of = {}
        wt_of = {}

        def wturn(n, tp=("acc", 7)):
            wt_of[n] = turn_words(wraw[:, n, :].bitcast(F32), tp)

        def wcopy(n, eng):
            b, al = divmod(n, 4)
            if al == 0:
                wg_of[b] = ring(rings, "wg", 2, [P, 2, 512, 2], F32, 64)
            dst = wg_of[b][:, :, P * al:P * (al + 1), :]
            src = wt_of[n][:].rearrange("p c u r -> p c r u")
            if eng == "S":
                nc.scalar.copy(out=dst, in_=src)
            else:
                nc.vector.tensor_copy(out=dst, in_=src)

        def wquant(b):
            wg = wg_of[b]
            for c in range(2):
                cols = slice(512 * b, 512 * (b + 1))
                nc.vector.quantize_mx(out=wc[:, c, cols].bitcast(FP8X4), scales=wsc[:, c, cols],
                                      in_=wg[:, c].rearrange("p f u -> p (f u)").bitcast(BF16))

        xs_of = {}
        xt_of = {}
        xg_of = {}

        def cast(g, i):
            xs_of[g, i] = ring(rings, "xs", 4, [P, D], BF16)
            if g == 2:
                nc.vector.tensor_copy(out=xs_of[g, i][:], in_=xb[:, g, D * i:D * (i + 1)].bitcast(FP8))
            else:
                nc.scalar.copy(out=xs_of[g, i][:], in_=xb[:, g, D * i:D * (i + 1)].bitcast(FP8))

        def turn(g, i):
            t = ring(banks, "tp", 1, [P, 2, 2, P], F32) if g >= 3 or (g == 2 and i == 0) else ring(banks, "acc", 7, [P, 2, 2, P], F32)
            words = xs_of[g, i][:].bitcast(F32)
            for c in range(2):
                for u in range(2):
                    nc.tensor.transpose(t[:, u, c, :], words[:, 256 * c + u:256 * (c + 1):2], ident[:])
            xt_of[g, i] = t

        def gather(g, i):
            if g not in xg_of:
                xg_of[g] = ring(rings, "xg", 2, [P, 2, 2, P, 4], BF16, 64)
            xg = xg_of[g]
            t = xt_of[g, i]
            nc.vector.tensor_tensor(
                out=xg[:, i].rearrange("p c r (u e) -> p c r u e", u=2),
                in0=scale_t[:].rearrange("p c (u e) -> p c u e", u=2).unsqueeze(2).to_broadcast([P, 2, P, 2, 2]),
                in1=t[:].rearrange("p u c r -> p (u c r)").bitcast(BF16).rearrange("p (u c r e) -> p c r u e", u=2, c=2, e=2),
                op=ALU.mult)

        def quant(xg):
            xc = ring(rings, "xc", 4, [P, 512], U32, 64)
            xsc = ring(rings, "xsc", 4, [P, 512], U8, 64)
            nc.vector.quantize_mx(out=xc[:].bitcast(FP8X4), scales=xsc[:],
                                  in_=xg[:].rearrange("p i c r t -> p (i c r t)"))
            return xc, xsc

        q_dst = [out_0[bt].rearrange("h (a p i) d -> a p h (i d)", a=4, p=P, i=2) for bt in range(2)]
        k_dst = [out_1[bt].rearrange("h (a p i) d -> a p h (i d)", a=4, p=P, i=2) for bt in range(2)]
        v_dst = [out_2[bt].rearrange("h (a p i) d -> a p h (i d)", a=4, p=P, i=2) for bt in range(2)]
        xq = {}
        acc_of = {}
        ss_of = {}
        nrm_of = {}
        nrme_of = {}
        rinv_of = {}
        o_of = {}
        pr_of = {}
        r_of = {}
        ov_of = {}

        def where(j):
            g, b = (j % 2, j // 2) if j < 6 else divmod(j, 3)
            return g, b, (4 if b < 2 else 2)

        def mx(j, i):
            g, b, nh = where(j)
            xc, xsc = xq[g]
            acc = ring(banks, "acc", 7, [P, 512], F32)
            for c in range(2):
                lc = slice(256 * i + P * c, 256 * i + P * (c + 1))
                rc = slice(512 * b, 512 * (b + 1))
                nc.tensor.matmul_mx(out=acc[:], lhsT=xc[:, lc].bitcast(FP8X4), lhsT_scale=xsc[:, lc],
                                    rhs=wc[:, c, rc].bitcast(FP8X4), rhs_scale=wsc[:, c, rc],
                                    start=(c == 0), stop=(c == 1))
            acc_of[j, i] = acc

        def squares(j, i):
            g, b, nh = where(j)
            if i == 0:
                ss_of[j] = ss_early[:, 8 * j:8 * j + 8] if j < 2 else ring(rings, "ss", 4, [P, 8], F32)[:]
            for h in range(nh):
                junk = ring(rings, "junk", 4, [P, HD], BF16)
                nc.scalar.activation(out=junk[:], in_=acc_of[j, i][:, HD * h:HD * (h + 1)], func=ACT.Square,
                                     accum_out=ss_of[j][:, i * nh + h:i * nh + h + 1])

        ss_early = keep.tile([P, 16], F32, name="ss_early")
        nrm_early = keep.tile([P, 16], F32, name="nrm_early")
        nrme_early = keep.tile([P, 16], F32, name="nrme_early")
        rinv_early = keep.tile([P, 16], F32, name="rinv_early")

        def early_norms():
            nc.scalar.activation(out=nrm_early[:], in_=ss_early[:], func=ACT.Sqrt)
            nc.scalar.activation(out=nrme_early[:], in_=nrm_early[:], func=ACT.Copy, bias=EPS)

        def early_invert():
            nc.vector.reciprocal(out=rinv_early[:], in_=nrme_early[:])

        def scaling(n):
            h, i, j = n % 4, n // 4 % 2, n // 8
            nc.scalar.activation(out=o_of[j][:, h, i, :], in_=r_of[j][:, h, i, :], func=ACT.Copy,
                                 scale=rinv_early[:, n // 4 * 4 + h:n // 4 * 4 + h + 1])

        def rescale(j):
            for i in range(2):
                for h in range(4):
                    nc.scalar.activation(out=o_of[j][:, h, i, :], in_=r_of[j][:, h, i, :], func=ACT.Copy,
                                         scale=rinv_of[j][:, i * 4 + h:i * 4 + h + 1])

        def vcopy(j):
            g, b, nh = where(j)
            if b == 2:
                ov = ring(rings, "ov", 2, [P, 2, 2, HD], F32)
                for i in range(2):
                    nc.scalar.copy(out=ov[:, :, i, :], in_=acc_of[j, i][:, 256:512].rearrange("p (h d) -> p h d", d=HD))
                ov_of[j] = ov

        def root(j):
            n = 2 * where(j)[2]
            nrm_of[j] = ring(rings, "nrm", 4, [P, 8], F32)
            nc.scalar.activation(out=nrm_of[j][:, 0:n], in_=ss_of[j][:, 0:n], func=ACT.Sqrt)

        def plus_eps(j):
            n = 2 * where(j)[2]
            nrme_of[j] = ring(rings, "nrme", 4, [P, 8], F32)
            nc.scalar.activation(out=nrme_of[j][:, 0:n], in_=nrm_of[j][:, 0:n], func=ACT.Copy, bias=EPS)

        def invert(j):
            n = 2 * where(j)[2]
            rinv_of[j] = ring(rings, "rinv", 7, [P, 8], F32)
            nc.vector.reciprocal(out=rinv_of[j][:, 0:n], in_=nrme_of[j][:, 0:n])

        def UNF(j):
            return j < 2

        def folded(j):
            return not UNF(j)

        def products(j, i):
            g, b, nh = where(j)
            if i == 0:
                pr_of[j] = ring(rings, "pr", 5, [P, 4, 2, 4, HALF], F32)
            pr = pr_of[j]
            if True:
                gi = 2 * (g % 4) + i
                acc = acc_of[j, i]
                table = rope[:, b // 2, gi].rearrange("p (d s) j -> p d (s j)", d=2)
                if folded(j):
                    for h in range(nh):
                        nc.vector.scalar_tensor_tensor(
                            out=pr[:, h, i].rearrange("p (d s) j -> p d (s j)", d=2),
                            in0=acc[:, HD * h:HD * (h + 1)].unsqueeze(1).to_broadcast([P, 2, HD]),
                            scalar=rinv_of[j][:, i * nh + h:i * nh + h + 1], in1=table, op0=ALU.mult, op1=ALU.mult)
                else:
                    nc.vector.tensor_tensor(
                        out=pr[:, 0:nh, i].rearrange("p h (d s) j -> p h d (s j)", d=2),
                        in0=table.unsqueeze(1).to_broadcast([P, nh, 2, HD]),
                        in1=acc[:, 0:nh * HD].rearrange("p (h d) -> p h d", d=HD).unsqueeze(2).to_broadcast([P, nh, 2, HD]),
                        op=ALU.mult)

        def adds_pair(j):
            g, b, nh = where(j)
            o_of[j] = ring(rings, "o", 6, [P, 4, 2, HD], F32)
            pv = pr_of[j][:, 0:nh].rearrange("p h i (d s) j -> p (h i d) s j", s=2)
            nc.gpsimd.tensor_tensor(out=o_of[j][:, 0:nh].rearrange("p h i (d j) -> p (h i d) j", d=2),
                                    in0=pv[:, :, 0, :], in1=pv[:, :, 1, :], op=ALU.add)

        def adds(j, i):
            g, b, nh = where(j)
            if i == 0:
                o_of[j] = ring(rings, "o", 6, [P, 4, 2, HD], F32) if j > 1 else keep.tile([P, 4, 2, HD], F32, name="o_early%d" % j)
                if not folded(j):
                    r_of[j] = ring(rings, "r", 3, [P, 4, 2, HD], F32) if j > 1 else keep.tile([P, 4, 2, HD], F32, name="r_early%d" % j)
            r = o_of[j] if folded(j) else r_of[j]
            pv = pr_of[j][:, 0:nh, i].rearrange("p h (d s) j -> p h d s j", s=2)
            eng = nc.vector if j == PAIRS - 1 or (j == PAIRS - 2 and i == 1) else nc.gpsimd
            eng.tensor_tensor(out=r[:, 0:nh, i, :].rearrange("p h (d j) -> p h d j", d=2),
                              in0=pv[:, :, :, 0, :], in1=pv[:, :, :, 1, :], op=ALU.add)

        def vstore(j):
            g, b, nh = where(j)
            if b == 2:
                bt, a = divmod(g, 4)
                nc.sync.dma_start(out=v_dst[bt][a], in_=ov_of[j][:].rearrange("p h i d -> p h (i d)"))

        def store(j):
            g, b, nh = where(j)
            o = o_of[j]
            bt, a = divmod(g, 4)
            ov = o[:].rearrange("p h i d -> p h (i d)")
            if b < 2:
                nc.sync.dma_start(out=q_dst[bt][a][:, 4 * b:4 * (b + 1), :], in_=ov)
            else:
                nc.sync.dma_start(out=k_dst[bt][a], in_=ov[:, 0:2, :])

        def xwork(j, slot):
            for g in range(3, GROUPS):
                for what, when in XPLAN:
                    if when == 4 * (j - 3 * g) + slot:
                        what(g)

        def xquant(g):
            xq[g] = quant(xg_of[g])

        XPLAN = ((lambda g: cast(g, 0), -30), (lambda g: cast(g, 1), -26), (lambda g: turn(g, 0), -25), (lambda g: gather(g, 0), -21),
                 (lambda g: turn(g, 1), -21), (lambda g: gather(g, 1), -17), (lambda g: xquant(g), -13))

        angles(((0, 2), (2, 8)))
        cast(0, 0)
        cast(0, 1)
        gam_copy()
        wturn(0)
        wcopy(0, "S")
        sines(0, 2)
        gains(0, 2, 0)
        wturn(1)
        turn(0, 0)
        turn(0, 1)
        wturn(2)
        wturn(3)
        wturn(4)
        wturn(5)
        wcopy(1, "S")
        gather(0, 0)
        wcopy(2, "S")
        gather(0, 1)
        wcopy(3, "S")
        cast(1, 0)
        turn(1, 0)
        cast(1, 1)
        wcopy(4, "S")
        xq[0] = quant(xg_of[0])
        wquant(0)
        mx(0, 0)
        mx(0, 1)
        turn(1, 1)
        wturn(6)
        wturn(7)
        for n in range(8, 12):
            wturn(n)
        sines(2, 8)
        gains(2, 4, 0)
        gains(4, 8, 0)
        wcopy(5, "S")
        gather(1, 0)
        products(0, 0)
        adds(0, 0)
        products(0, 1)
        adds(0, 1)
        squares(0, 0)
        squares(0, 1)
        gather(1, 1)
        wcopy(6, "S")
        wcopy(7, "S")
        wcopy(8, "S")
        wcopy(9, "S")
        xq[1] = quant(xg_of[1])
        cast(2, 0)
        wquant(1)
        cast(2, 1)
        mx(1, 0)
        mx(1, 1)
        mx(2, 0)
        mx(2, 1)
        squares(1, 0)
        squares(1, 1)
        nc.scalar.activation(out=first[:, 1:2], in_=sin2[:, 7, 1, 0:1], func=ACT.Sqrt, scale=0.0, bias=1.0)
        products(1, 0)
        adds(1, 0)
        products(1, 1)
        adds(1, 1)
        gains(0, 2, 1)
        gains(2, 4, 1)
        gains(4, 8, 1)
        squares(2, 0)
        squares(2, 1)
        root(2)
        turn(2, 0)
        turn(2, 1)
        plus_eps(2)
        wcopy(10, "S")
        wcopy(11, "S")
        gather(2, 0)
        gather(2, 1)
        invert(2)
        mx(3, 0)
        mx(3, 1)
        products(2, 0)
        adds(2, 0)
        products(2, 1)
        adds(2, 1)
        squares(3, 0)
        squares(3, 1)
        root(3)
        wquant(2)
        xq[2] = quant(xg_of[2])
        mx(4, 0)
        mx(4, 1)
        mx(5, 0)
        mx(5, 1)
        plus_eps(3)
        invert(3)
        for s in range(-8, 8):
            xwork(s // 4, s % 4)
        products(3, 0)
        adds(3, 0)
        products(3, 1)
        adds(3, 1)
        squares(4, 0)
        squares(4, 1)
        root(4)
        vcopy(4)
        plus_eps(4)
        vstore(4)
        for s in range(8, 12):
            xwork(s // 4, s % 4)
        mx(6, 0)
        mx(6, 1)
        mx(7, 0)
        invert(4)
        squares(5, 0)
        squares(5, 1)
        root(5)
        vcopy(5)
        plus_eps(5)
        vstore(5)
        squares(6, 0)
        store(2)
        store(3)

        for j in range(4, PAIRS + 1):
            if j + 3 < PAIRS and j > 4:
                mx(j + 3, 0)
            if j + 2 < PAIRS:
                squares(j + 2, 1)
            xwork(j, 0)
            if j < PAIRS:
                products(j, 0)
                if not (lambda n: n % 3 == 2 and n < 23)(j):
                    adds(j, 0)
            if j == 4:
                for s in range(12, 16):
                    xwork(s // 4, s % 4)
            xwork(j, 1)
            if j + 3 < PAIRS:
                mx(j + 3, 1)
                squares(j + 3, 0)
            if j + 2 < PAIRS:
                root(j + 2)
                vcopy(j + 2)
            pass
            if j + 2 < PAIRS:
                plus_eps(j + 2)
                vstore(j + 2)
            xwork(j, 2)
            if j - 2 > 1 and j - 2 < PAIRS and not folded(j - 2):
                rescale(j - 2)
                store(j - 2)
            if j == 5:
                early_norms()
            if j == 7:
                early_invert()
            if j in (9, 15):
                u = (j - 9) // 6
                for n in range(8):
                    scaling(8 * u + n)
                store(u)
            if j + 1 < PAIRS:
                invert(j + 1)
            if j < PAIRS:
                products(j, 1)
                if (lambda n: n % 3 == 2 and n < 23)(j):
                    adds_pair(j)
                else:
                    adds(j, 1)
            xwork(j, 3)
            if j > 4 and folded(j - 1):
                store(j - 1)
